import numpy as np
import ml_dtypes


def mxq(x, axis, fmt="e4m3"):
    dtype, down = {"e4m3": (ml_dtypes.float8_e4m3fn, 7), "e5m2": (ml_dtypes.float8_e5m2, 14)}[fmt]
    v = np.moveaxis(np.asarray(x, np.float32).astype(ml_dtypes.bfloat16).astype(np.float64), axis, -1)
    blocks = v.reshape(v.shape[:-1] + (-1, 32))
    amax = np.abs(blocks).max(-1, keepdims=True)
    byte = np.maximum(np.where(amax > 0, np.frexp(amax)[1] - 1 + 127, 0) - down, 1)
    scale = np.exp2(byte - 127.0)
    codes = (blocks / scale).astype(np.float32).astype(dtype).astype(np.float64)
    return np.moveaxis((codes * scale).reshape(v.shape), -1, axis)


WIDE = False


def mx_kscale(k):
    if not WIDE:
        return np.ones(k)
    levels = np.array([10, -10, 5, -5, 0])
    if k % 512:
        return np.exp2(np.random.permutation(np.resize(levels, k // 32))).repeat(32)
    a = np.empty((k // 512, 16))
    for p in range(k // 512):
        a[p, :8] = np.random.permutation(np.resize(levels, 8))
        for g in range(8):
            far = levels[np.abs(levels - a[p, g]) >= 10]
            a[p, g + 8] = far[np.random.randint(len(far))]
    return np.exp2(a.ravel()).repeat(32)


BF16 = ml_dtypes.bfloat16


def bf(x):
    return np.asarray(x, np.float32).astype(BF16)


def f64(x):
    return np.asarray(x).astype(np.float64)


B, T, D = 8, 512, 256
GAMMA = 0.5
EPS = 1e-06
REL_THRESH = 1e-09


def setup_inputs():
    s = mx_kscale(T)
    a = np.random.uniform(0.0, 1.0, (B, T, T))
    a = 0.5 * (a + a.transpose(0, 2, 1))
    k = np.random.standard_normal((B, T, D)) * np.sqrt(T)
    return {"A_rel": bf(a * s), "k_seq": bf(k * np.mean(s) / s[:, None])}


def reference(A_rel, k_seq):
    A = f64(A_rel)
    deg = np.sum(A, axis=-1) + EPS
    d_inv_sqrt = 1.0 / np.sqrt(deg)
    W = A * d_inv_sqrt[:, :, None] * d_inv_sqrt[:, None, :]
    n = A.shape[1]
    tril = np.tril(np.ones((n, n)))
    W_causal = W * tril
    a = mxq(W_causal, 2, "e4m3") @ mxq(f64(k_seq), 1, "e4m3")
    has_relation = np.max(np.abs(W) * tril, axis=-1) > REL_THRESH
    a_scaled = a * np.sqrt(GAMMA)
    out = a_scaled * has_relation[:, :, None].astype(np.float64)
    return out

@@ -1,0 +1,277 @@
+import math
+from contextlib import ExitStack
+
+import concourse.mybir as mybir
+from concourse.masks import make_identity
+
+F32 = mybir.dt.float32
+BF16 = mybir.dt.bfloat16
+I32 = mybir.dt.int32
+U32 = mybir.dt.uint32
+U8 = mybir.dt.uint8
+FP8X4 = mybir.dt.float8_e4m3fn_x4
+ALU = mybir.AluOpType
+ACT = mybir.ActivationFunctionType
+
+B, T, D = 8, 512, 256
+P = 128
+NB = T // P
+PACK = 4
+GAMMA = 0.5
+EPS = 1e-06
+REL_THRESH = 1e-09
+FLOPS = 2 * B * T * T * D
+
+DIAG_STEP = T + P
+N_W = 3
+K_ON_VECTOR = 2
+
+
+def tile_symbolicpenaltytracker_kernel(tc, A_rel, k_seq, out):
+    nc = tc.nc
+    with ExitStack() as ctx:
+        const = ctx.enter_context(tc.tile_pool(name="const", bufs=1))
+        resid = ctx.enter_context(tc.tile_pool(name="resid", bufs=1))
+        small = ctx.enter_context(tc.tile_pool(name="small", bufs=4))
+        work = ctx.enter_context(tc.tile_pool(name="work", bufs=3))
+        ps_dis = ctx.enter_context(tc.psum_pool(name="ps_dis", bufs=2))
+        ps_thr = ctx.enter_context(tc.psum_pool(name="ps_thr", bufs=1))
+        ps_wt = ctx.enter_context(tc.psum_pool(name="ps_wt", bufs=3))
+        ps_out = ctx.enter_context(tc.psum_pool(name="ps_out", bufs=2))
+
+        a_sb = [resid.tile([P, NB * DIAG_STEP], BF16, name="a%d" % b) for b in range(B)]
+        k_sb = [resid.tile([P, PACK, D], BF16, name="k%d" % b) for b in range(B)]
+
+        def rows(b):
+            return a_sb[b][:, 0 : NB * T].rearrange("p (i s) -> p i s", s=T)
+
+        def load_a(b):
+            if b == 0:
+                for i in range(NB):
+                    nc.sync.dma_start(out=rows(b)[:, i, :], in_=A_rel[b, i * P : (i + 1) * P, :])
+            else:
+                nc.sync.dma_start(out=rows(b), in_=A_rel[b].rearrange("(i p) s -> p i s", p=P))
+
+        def load_k(b):
+            nc.sync.dma_start(out=k_sb[b][:], in_=k_seq[b].rearrange("(p u) d -> p u d", u=PACK))
+
+        load_a(0)
+        for b in range(K_ON_VECTOR):
+            load_k(b)
+        for b in range(1, B):
+            load_a(b)
+            if b >= K_ON_VECTOR:
+                load_k(b)
+
+        warm = const.tile([P, 1], F32, name="warm")
+        nc.vector.memset(warm[:], 1.0)
+        nc.scalar.activation(out=warm[:], in_=warm[:], func=ACT.Sqrt)
+
+        w_tiles = []
+        for j in range(N_W):
+            w = const.tile([P, NB * T], BF16, name="w%d" % j, align_bytes=64)
+            nc.vector.memset(w[:].bitcast(I32), 0)
+            w_tiles.append(w)
+
+        tril_f = const.tile([P, P], F32, name="tril_f")
+        nc.gpsimd.memset(tril_f[:], 1.0)
+        nc.gpsimd.affine_select(
+            out=tril_f[:], in_=tril_f[:], compare_op=ALU.is_ge, fill=0.0, base=0,
+            pattern=[[-1, P]], channel_multiplier=1,
+        )
+        ident_f = const.tile([P, P], F32, name="ident_f")
+        make_identity(nc, ident_f[:])
+        tril = const.tile([P, P], BF16, name="tril")
+        nc.vector.tensor_copy(out=tril[:], in_=tril_f[:])
+
+        state = {}
+        k_codes = {}
+
+        def prepare_k(b):
+            kg = work.tile([P, D * PACK], BF16, name="kg", align_bytes=64)
+            if b < K_ON_VECTOR:
+                nc.vector.tensor_copy(
+                    out=kg[:].rearrange("p (c i u) -> p c u i", i=4, u=PACK),
+                    in_=k_sb[b][:].rearrange("p u (c i) -> p c u i", i=4),
+                )
+            else:
+                nc.gpsimd.tensor_scalar(
+                    out=kg[:].rearrange("p (d u) -> p d u", u=PACK),
+                    in0=k_sb[b][:].rearrange("p u d -> p d u"),
+                    scalar1=1.0, scalar2=0.0, op0=ALU.mult, op1=ALU.add,
+                )
+            codes = resid.tile([P, D], U32, name="kc%d" % b, align_bytes=64)
+            scales = resid.tile([P, D], U8, name="ks%d" % b, align_bytes=64)
+            nc.vector.quantize_mx(out=codes[:].bitcast(FP8X4), scales=scales[:], in_=kg[:])
+            k_codes[b] = (codes, scales)
+
+        ALL = list(range(NB))
+
+        def row_sums(b, blocks):
+            if b not in state:
+                state[b] = {
+                    "deg": small.tile([P, NB], F32, name="deg"),
+                    "sd": small.tile([P, NB], F32, name="sd"),
+                    "thr": small.tile([P, NB], F32, name="thr"),
+                }
+            s = state[b]
+            for i in blocks:
+                unused = work.tile([P, T], BF16, name="unused")
+                nc.scalar.activation(
+                    out=unused[:], in_=rows(b)[:, i, :], func=ACT.Copy, accum_out=s["deg"][:, i : i + 1]
+                )
+            c = slice(blocks[0], blocks[-1] + 1)
+            nc.scalar.activation(out=s["sd"][:, c], in_=s["deg"][:, c], func=ACT.Sqrt, bias=EPS)
+            nc.scalar.mul(out=s["thr"][:, c], in_=s["sd"][:, c], mul=REL_THRESH)
+
+        def scales(b, blocks):
+            s = state[b]
+            if "dis" not in s:
+                s["dis"] = small.tile([P, NB], F32, name="dis")
+            c = slice(blocks[0], blocks[-1] + 1)
+            nc.vector.reciprocal(out=s["dis"][:, c], in_=s["sd"][:, c])
+
+        def mask_and_abs(b, blocks):
+            s = state[b]
+            if "abs" not in s:
+                s["abs"] = work.tile([P, NB * T], BF16, name="a_abs")
+            a_words = a_sb[b][:, 0 : NB * T].bitcast(I32)
+            abs_words = s["abs"][:].bitcast(I32)
+            if len(blocks) == 1:
+                i = blocks[0]
+                n = (i + 1) * P
+                diag = rows(b)[:, i, i * P : n]
+                nc.vector.tensor_tensor(out=diag, in0=diag, in1=tril[:], op=ALU.mult)
+                w0 = i * (T // 2)
+                nc.vector.tensor_single_scalar(
+                    out=abs_words[:, w0 : w0 + n // 2], in_=a_words[:, w0 : w0 + n // 2],
+                    scalar=0x7FFF7FFF, op=ALU.bitwise_and,
+                )
+            else:
+                diag = a_sb[b][:].rearrange("p (i x) -> p i x", x=DIAG_STEP)[:, :, 0:P]
+                nc.vector.tensor_tensor(
+                    out=diag, in0=diag, in1=tril[:].unsqueeze(1).to_broadcast([P, NB, P]), op=ALU.mult
+                )
+                nc.vector.tensor_single_scalar(out=abs_words, in_=a_words, scalar=0x7FFF7FFF, op=ALU.bitwise_and)
+
+        def spread(b, blocks):
+            s = state[b]
+            if "dis_all" not in s:
+                s["dis_all"] = ps_dis.tile([P, T], F32, name="dis_all")
+                s["thr_all"] = ps_thr.tile([P, T], F32, name="thr_all")
+            for dst, src in ((s["dis_all"], s["dis"]), (s["thr_all"], s["thr"])):
+                for i in blocks:
+                    nc.tensor.transpose(
+                        out=dst[:, i * P : (i + 1) * P],
+                        in_=src[:, i : i + 1].to_broadcast([P, P]),
+                        identity=ident_f[:],
+                    )
+
+        def weights(b, i):
+            s = state[b]
+            w = w_tiles[b % N_W]
+            if "grouped" not in s:
+                s["grouped"] = work.tile([P, NB * P * PACK], BF16, name="grouped", align_bytes=64)
+            if i in (3, 2) and "wt_hi" not in s:
+                s["wt_hi"] = ps_wt.tile([P, 2, 2, P], F32, name="wt")
+            if i in (1, 0) and "wt_lo" not in s:
+                s["wt_lo"] = ps_wt.tile([P, 2, 2, P], F32, name="wt")
+            n = (i + 1) * P
+            nc.vector.scalar_tensor_tensor(
+                out=w[:, i * T : i * T + n], in0=rows(b)[:, i, 0:n], scalar=s["dis"][:, i : i + 1],
+                in1=s["dis_all"][:, 0:n], op0=ALU.mult, op1=ALU.mult,
+            )
+            words = w[:, i * T : (i + 1) * T].bitcast(F32)
+            wt = s["wt_hi" if i >= 2 else "wt_lo"]
+            for v in range(2):
+                nc.tensor.transpose(out=wt[:, i % 2, v, :], in_=words[:, v::2], identity=ident_f[:])
+            g = s["grouped"][:].bitcast(F32).rearrange("p (i t v) -> p i t v", t=P, v=2)
+            nc.scalar.copy(out=g[:, i, :, :], in_=wt[:, i % 2, :, :].rearrange("p v t -> p t v"))
+
+        def count(b, i):
+            s = state[b]
+            if "cnt" not in s:
+                s["cnt"] = small.tile([P, NB], F32, name="cnt")
+            n = (i + 1) * P
+            hits = work.tile([P, T], BF16, name="hits")
+            nc.vector.scalar_tensor_tensor(
+                out=hits[:, 0:n], in0=s["abs"][:].rearrange("p (i s) -> p i s", s=T)[:, i, 0:n],
+                scalar=s["dis"][:, i : i + 1], in1=s["thr_all"][:, 0:n],
+                op0=ALU.mult, op1=ALU.is_gt, accum_out=s["cnt"][:, i : i + 1],
+            )
+
+        def factor(b):
+            s = state[b]
+            s["fac"] = small.tile([P, NB], F32, name="fac")
+            engine = nc.vector if b == B - 1 else nc.gpsimd
+            engine.tensor_scalar(
+                out=s["fac"][:], in0=s["cnt"][:], scalar1=0.5, scalar2=math.sqrt(GAMMA),
+                op0=ALU.is_gt, op1=ALU.mult,
+            )
+
+        def product(b):
+            s = state[b]
+            g = s["grouped"]
+            kc, ks = k_codes[b]
+            last = b == B - 1
+            codes = work.tile([P, NB * P], U32, name="wc", align_bytes=64)
+            scl = work.tile([P, NB * P], U8, name="ws", align_bytes=64)
+            res = work.tile([P, NB, D], F32, name="res")
+            dst = out[b].rearrange("(i p) d -> p i d", p=P)
+            if not last:
+                nc.vector.quantize_mx(out=codes[:].bitcast(FP8X4), scales=scl[:], in_=g[:])
+            for h in (1, 0):
+                if last:
+                    c = slice(h * 2 * P, (h + 1) * 2 * P)
+                    nc.vector.quantize_mx(
+                        out=codes[:, c].bitcast(FP8X4), scales=scl[:, c],
+                        in_=g[:, h * 2 * P * PACK : (h + 1) * 2 * P * PACK],
+                    )
+                acc = ps_out.tile([P, 2, D], F32, name="acc")
+                for j in range(2):
+                    c = slice((2 * h + j) * P, (2 * h + j + 1) * P)
+                    nc.tensor.matmul_mx(
+                        out=acc[:, j, :],
+                        lhsT=codes[:, c].bitcast(FP8X4), lhsT_scale=scl[:, c],
+                        rhs=kc[:].bitcast(FP8X4), rhs_scale=ks[:],
+                        start=True, stop=True,
+                    )
+                for j in range(2):
+                    i = 2 * h + j
+                    if last and j == 1:
+                        nc.vector.tensor_scalar_mul(out=res[:, i, :], in0=acc[:, j, :], scalar1=s["fac"][:, i : i + 1])
+                    else:
+                        nc.scalar.activation(
+                            out=res[:, i, :], in_=acc[:, j, :], func=ACT.Copy, scale=s["fac"][:, i : i + 1]
+                        )
+                if last:
+                    nc.sync.dma_start(out=dst[:, 2 * h : 2 * h + 2, :], in_=res[:, 2 * h : 2 * h + 2, :])
+            if not last:
+                nc.sync.dma_start(out=dst, in_=res[:])
+
+        for i in ALL:
+            row_sums(0, [i])
+            scales(0, [i])
+            mask_and_abs(0, [i])
+            spread(0, [i])
+            weights(0, i)
+            count(0, i)
+        factor(0)
+        for b in range(K_ON_VECTOR):
+            prepare_k(b)
+        for b in range(1, B + 2):
+            if b < B:
+                row_sums(b, ALL)
+                scales(b, ALL)
+                mask_and_abs(b, ALL)
+                spread(b, ALL)
+                if b >= K_ON_VECTOR:
+                    prepare_k(b)
+            if 1 <= b - 1 < B:
+                for i in reversed(ALL):
+                    weights(b - 1, i)
+                for i in reversed(ALL):
+                    count(b - 1, i)
+                factor(b - 1)
+            if b - 2 >= 0:
+                product(b - 2)

@@ -12,19 +12,25 @@ U8 = mybir.dt.uint8
 FP8X4 = mybir.dt.float8_e4m3fn_x4
 ALU = mybir.AluOpType
 ACT = mybir.ActivationFunctionType
+AX = mybir.AxisListType
 
 B, T, D = 8, 512, 256
 P = 128
 NB = T // P
 PACK = 4
+Q = P // PACK
 GAMMA = 0.5
 EPS = 1e-06
 REL_THRESH = 1e-09
 FLOPS = 2 * B * T * T * D
 
 DIAG_STEP = T + P
-N_W = 3
 K_ON_VECTOR = 2
+N_KA = 3
+N_KB = 2
+W_FIRST = {3: 0, 2: 512, 0: 896, 1: 1024}
+W_MAIN = 1024
+W_ALL = 1280
 
 
 def tile_symbolicpenaltytracker_kernel(tc, A_rel, k_seq, out):
@@ -35,9 +41,8 @@ def tile_symbolicpenaltytracker_kernel(tc, A_rel, k_seq, out):
         small = ctx.enter_context(tc.tile_pool(name="small", bufs=4))
         work = ctx.enter_context(tc.tile_pool(name="work", bufs=3))
         ps_dis = ctx.enter_context(tc.psum_pool(name="ps_dis", bufs=2))
-        ps_thr = ctx.enter_context(tc.psum_pool(name="ps_thr", bufs=1))
-        ps_wt = ctx.enter_context(tc.psum_pool(name="ps_wt", bufs=3))
-        ps_out = ctx.enter_context(tc.psum_pool(name="ps_out", bufs=2))
+        ps_wt = ctx.enter_context(tc.psum_pool(name="ps_wt", bufs=1))
+        ps_out = ctx.enter_context(tc.psum_pool(name="ps_out", bufs=3))
 
         a_sb = [resid.tile([P, NB * DIAG_STEP], BF16, name="a%d" % b) for b in range(B)]
         k_sb = [resid.tile([P, PACK, D], BF16, name="k%d" % b) for b in range(B)]
@@ -67,12 +72,6 @@ def tile_symbolicpenaltytracker_kernel(tc, A_rel, k_seq, out):
         nc.vector.memset(warm[:], 1.0)
         nc.scalar.activation(out=warm[:], in_=warm[:], func=ACT.Sqrt)
 
-        w_tiles = []
-        for j in range(N_W):
-            w = const.tile([P, NB * T], BF16, name="w%d" % j, align_bytes=64)
-            nc.vector.memset(w[:].bitcast(I32), 0)
-            w_tiles.append(w)
-
         tril_f = const.tile([P, P], F32, name="tril_f")
         nc.gpsimd.memset(tril_f[:], 1.0)
         nc.gpsimd.affine_select(
@@ -84,8 +83,23 @@ def tile_symbolicpenaltytracker_kernel(tc, A_rel, k_seq, out):
         tril = const.tile([P, P], BF16, name="tril")
         nc.vector.tensor_copy(out=tril[:], in_=tril_f[:])
 
-        state = {}
-        k_codes = {}
+        kc = [const.tile([P, D], U32, name="kc%d" % b, align_bytes=64) for b in range(B)]
+        ks = const.tile([P, B, D], U8, name="ks", align_bytes=64)
+        nc.vector.memset(ks[:].rearrange("p b d -> p (b d)").bitcast(I32), 0)
+        ka = [const.tile([P, 2, D], U32, name="ka%d" % j, align_bytes=64) for j in range(N_KA)]
+        ka_s = [const.tile([P, 2, D], U8, name="ka_s%d" % j, align_bytes=64) for j in range(N_KA)]
+        kb = [const.tile([P, 2, D], U32, name="kb%d" % j, align_bytes=64) for j in range(N_KB)]
+        kb_s = [const.tile([P, 2, D], U8, name="kb_s%d" % j, align_bytes=64) for j in range(N_KB)]
+        for t in ka + kb + ka_s + kb_s:
+            nc.vector.memset(t[:].rearrange("p h d -> p (h d)").bitcast(I32), 0)
+
+        state = [{} for b in range(B)]
+        ALL = list(range(NB))
+
+        def tile_of(b, name, make):
+            if name not in state[b]:
+                state[b][name] = make()
+            return state[b][name]
 
         def prepare_k(b):
             kg = work.tile([P, D * PACK], BF16, name="kg", align_bytes=64)
@@ -100,178 +114,189 @@ def tile_symbolicpenaltytracker_kernel(tc, A_rel, k_seq, out):
                     in0=k_sb[b][:].rearrange("p u d -> p d u"),
                     scalar1=1.0, scalar2=0.0, op0=ALU.mult, op1=ALU.add,
                 )
-            codes = resid.tile([P, D], U32, name="kc%d" % b, align_bytes=64)
-            scales = resid.tile([P, D], U8, name="ks%d" % b, align_bytes=64)
-            nc.vector.quantize_mx(out=codes[:].bitcast(FP8X4), scales=scales[:], in_=kg[:])
-            k_codes[b] = (codes, scales)
+            nc.vector.quantize_mx(out=kc[b][:].bitcast(FP8X4), scales=ks[:, b, :], in_=kg[:])
 
-        ALL = list(range(NB))
+            def move(dst, dst_s, half, p0, n):
+                nc.sync.dma_start(
+                    out=dst[p0 : p0 + n, half, :].bitcast(I32), in_=kc[b][0:n, :].bitcast(I32)
+                )
+                nc.sync.dma_start(
+                    out=dst_s[p0 : p0 + n, half, :].bitcast(I32), in_=ks[0:n, b, :].bitcast(I32)
+                )
+
+            j = b % N_KA
+            move(ka[j], ka_s[j], 0, 0, 3 * Q)
+            move(ka[j], ka_s[j], 1, 3 * Q, Q)
+            m = (b // 2) % N_KB
+            move(kb[m], kb_s[m], b % 2, (b % 2) * 2 * Q, 2 * Q)
 
         def row_sums(b, blocks):
-            if b not in state:
-                state[b] = {
-                    "deg": small.tile([P, NB], F32, name="deg"),
-                    "sd": small.tile([P, NB], F32, name="sd"),
-                    "thr": small.tile([P, NB], F32, name="thr"),
-                }
-            s = state[b]
+            deg = tile_of(b, "deg", lambda: small.tile([P, NB], F32, name="deg"))
+            sd = tile_of(b, "sd", lambda: small.tile([P, NB], F32, name="sd"))
+            dis = tile_of(b, "dis", lambda: small.tile([P, NB], F32, name="dis"))
             for i in blocks:
                 unused = work.tile([P, T], BF16, name="unused")
                 nc.scalar.activation(
-                    out=unused[:], in_=rows(b)[:, i, :], func=ACT.Copy, accum_out=s["deg"][:, i : i + 1]
+                    out=unused[:], in_=rows(b)[:, i, :], func=ACT.Copy, accum_out=deg[:, i : i + 1]
                 )
             c = slice(blocks[0], blocks[-1] + 1)
-            nc.scalar.activation(out=s["sd"][:, c], in_=s["deg"][:, c], func=ACT.Sqrt, bias=EPS)
-            nc.scalar.mul(out=s["thr"][:, c], in_=s["sd"][:, c], mul=REL_THRESH)
+            nc.scalar.activation(out=sd[:, c], in_=deg[:, c], func=ACT.Sqrt, bias=EPS)
+            nc.vector.reciprocal(out=dis[:, c], in_=sd[:, c])
 
-        def scales(b, blocks):
-            s = state[b]
-            if "dis" not in s:
-                s["dis"] = small.tile([P, NB], F32, name="dis")
-            c = slice(blocks[0], blocks[-1] + 1)
-            nc.vector.reciprocal(out=s["dis"][:, c], in_=s["sd"][:, c])
+        def spread(b, blocks):
+            dis_all = tile_of(b, "dis_all", lambda: ps_dis.tile([P, T], F32, name="dis_all"))
+            for i in blocks:
+                nc.tensor.transpose(
+                    out=dis_all[:, i * P : (i + 1) * P],
+                    in_=state[b]["dis"][:, i : i + 1].to_broadcast([P, P]),
+                    identity=ident_f[:],
+                )
 
-        def mask_and_abs(b, blocks):
-            s = state[b]
-            if "abs" not in s:
-                s["abs"] = work.tile([P, NB * T], BF16, name="a_abs")
-            a_words = a_sb[b][:, 0 : NB * T].bitcast(I32)
-            abs_words = s["abs"][:].bitcast(I32)
+        def mask(b, blocks):
             if len(blocks) == 1:
                 i = blocks[0]
-                n = (i + 1) * P
-                diag = rows(b)[:, i, i * P : n]
+                diag = rows(b)[:, i, i * P : (i + 1) * P]
                 nc.vector.tensor_tensor(out=diag, in0=diag, in1=tril[:], op=ALU.mult)
-                w0 = i * (T // 2)
-                nc.vector.tensor_single_scalar(
-                    out=abs_words[:, w0 : w0 + n // 2], in_=a_words[:, w0 : w0 + n // 2],
-                    scalar=0x7FFF7FFF, op=ALU.bitwise_and,
-                )
             else:
                 diag = a_sb[b][:].rearrange("p (i x) -> p i x", x=DIAG_STEP)[:, :, 0:P]
                 nc.vector.tensor_tensor(
                     out=diag, in0=diag, in1=tril[:].unsqueeze(1).to_broadcast([P, NB, P]), op=ALU.mult
                 )
-                nc.vector.tensor_single_scalar(out=abs_words, in_=a_words, scalar=0x7FFF7FFF, op=ALU.bitwise_and)
 
-        def spread(b, blocks):
-            s = state[b]
-            if "dis_all" not in s:
-                s["dis_all"] = ps_dis.tile([P, T], F32, name="dis_all")
-                s["thr_all"] = ps_thr.tile([P, T], F32, name="thr_all")
-            for dst, src in ((s["dis_all"], s["dis"]), (s["thr_all"], s["thr"])):
-                for i in blocks:
-                    nc.tensor.transpose(
-                        out=dst[:, i * P : (i + 1) * P],
-                        in_=src[:, i : i + 1].to_broadcast([P, P]),
-                        identity=ident_f[:],
-                    )
+        def w32(b, i):
+            return state[b]["w32"][:, W_FIRST[i] : W_FIRST[i] + (i + 1) * P]
 
-        def weights(b, i):
-            s = state[b]
-            w = w_tiles[b % N_W]
-            if "grouped" not in s:
-                s["grouped"] = work.tile([P, NB * P * PACK], BF16, name="grouped", align_bytes=64)
-            if i in (3, 2) and "wt_hi" not in s:
-                s["wt_hi"] = ps_wt.tile([P, 2, 2, P], F32, name="wt")
-            if i in (1, 0) and "wt_lo" not in s:
-                s["wt_lo"] = ps_wt.tile([P, 2, 2, P], F32, name="wt")
+        def multiply(b, i):
+            tile_of(b, "w32", lambda: work.tile([P, W_ALL], F32, name="w32"))
             n = (i + 1) * P
             nc.vector.scalar_tensor_tensor(
-                out=w[:, i * T : i * T + n], in0=rows(b)[:, i, 0:n], scalar=s["dis"][:, i : i + 1],
-                in1=s["dis_all"][:, 0:n], op0=ALU.mult, op1=ALU.mult,
+                out=w32(b, i), in0=rows(b)[:, i, 0:n], scalar=state[b]["dis"][:, i : i + 1],
+                in1=state[b]["dis_all"][:, 0:n], op0=ALU.mult, op1=ALU.mult,
             )
-            words = w[:, i * T : (i + 1) * T].bitcast(F32)
-            wt = s["wt_hi" if i >= 2 else "wt_lo"]
-            for v in range(2):
-                nc.tensor.transpose(out=wt[:, i % 2, v, :], in_=words[:, v::2], identity=ident_f[:])
-            g = s["grouped"][:].bitcast(F32).rearrange("p (i t v) -> p i t v", t=P, v=2)
-            nc.scalar.copy(out=g[:, i, :, :], in_=wt[:, i % 2, :, :].rearrange("p v t -> p t v"))
 
-        def count(b, i):
+        def round_and_turn(b):
             s = state[b]
-            if "cnt" not in s:
-                s["cnt"] = small.tile([P, NB], F32, name="cnt")
-            n = (i + 1) * P
-            hits = work.tile([P, T], BF16, name="hits")
-            nc.vector.scalar_tensor_tensor(
-                out=hits[:, 0:n], in0=s["abs"][:].rearrange("p (i s) -> p i s", s=T)[:, i, 0:n],
-                scalar=s["dis"][:, i : i + 1], in1=s["thr_all"][:, 0:n],
-                op0=ALU.mult, op1=ALU.is_gt, accum_out=s["cnt"][:, i : i + 1],
+            w16 = work.tile([P, W_MAIN], BF16, name="w16", align_bytes=64)
+            nc.vector.tensor_copy(out=w16[:], in_=s["w32"][:, 0:W_MAIN])
+            even = b - b % 2
+            w16b = tile_of(even, "w16b", lambda: work.tile([P, 2, 2 * P], BF16, name="w16b", bufs=2, align_bytes=64))
+            nc.vector.tensor_copy(out=w16b[:, b % 2, :], in_=s["w32"][:, W_MAIN:W_ALL])
+            wt = ps_wt.tile([P, 2, 2, P], F32, name="wt", bufs=2)
+            words = w16[:].bitcast(F32)
+            for j in range(2):
+                for v in range(2):
+                    nc.tensor.transpose(
+                        out=wt[:, j, v, :], in_=words[:, j * 256 + v : (j + 1) * 256 : 2], identity=ident_f[:]
+                    )
+            grouped = work.tile([P, 2 * P * PACK], BF16, name="grouped", align_bytes=64)
+            s["grouped"] = grouped
+            nc.scalar.copy(
+                out=grouped[:].bitcast(F32).rearrange("p (j t v) -> p j t v", t=P, v=2),
+                in_=wt[:].rearrange("p j v t -> p j t v"),
+            )
+            if b % 2:
+                wtb = ps_wt.tile([P, 2, P], F32, name="wtb")
+                words = w16b[:].rearrange("p h s -> p (h s)").bitcast(F32)
+                for v in range(2):
+                    nc.tensor.transpose(out=wtb[:, v, :], in_=words[:, v::2], identity=ident_f[:])
+                groupedb = work.tile([P, P * PACK], BF16, name="groupedb", bufs=2, align_bytes=64)
+                s["groupedb"] = groupedb
+                nc.scalar.copy(
+                    out=groupedb[:].bitcast(F32).rearrange("p (t v) -> p t v", v=2),
+                    in_=wtb[:].rearrange("p v t -> p t v"),
+                )
+
+        def largest(b, i):
+            top = tile_of(b, "top", lambda: small.tile([P, NB], F32, name="top"))
+            nc.vector.tensor_reduce(
+                out=top[:, i : i + 1], in_=w32(b, i), axis=AX.X, op=ALU.max, apply_absolute_value=True
             )
 
         def factor(b):
-            s = state[b]
-            s["fac"] = small.tile([P, NB], F32, name="fac")
+            fac = tile_of(b, "fac", lambda: small.tile([P, NB], F32, name="fac"))
             engine = nc.vector if b == B - 1 else nc.gpsimd
             engine.tensor_scalar(
-                out=s["fac"][:], in0=s["cnt"][:], scalar1=0.5, scalar2=math.sqrt(GAMMA),
+                out=fac[:], in0=state[b]["top"][:], scalar1=REL_THRESH, scalar2=math.sqrt(GAMMA),
                 op0=ALU.is_gt, op1=ALU.mult,
             )
 
+        def scale_out(b, i, acc, engine):
+            res = tile_of(b, "res", lambda: work.tile([P, NB, D], F32, name="res", bufs=4))
+            fac = state[b]["fac"][:, i : i + 1]
+            if engine == "scalar":
+                nc.scalar.activation(out=res[:, i, :], in_=acc, func=ACT.Copy, scale=fac)
+            else:
+                nc.vector.tensor_scalar_mul(out=res[:, i, :], in0=acc, scalar1=fac)
+
+        def store(b, i0):
+            dst = out[b].rearrange("(i p) d -> p i d", p=P)
+            nc.sync.dma_start(out=dst[:, i0 : i0 + 2, :], in_=state[b]["res"][:, i0 : i0 + 2, :])
+
         def product(b):
             s = state[b]
-            g = s["grouped"]
-            kc, ks = k_codes[b]
             last = b == B - 1
-            codes = work.tile([P, NB * P], U32, name="wc", align_bytes=64)
-            scl = work.tile([P, NB * P], U8, name="ws", align_bytes=64)
-            res = work.tile([P, NB, D], F32, name="res")
-            dst = out[b].rearrange("(i p) d -> p i d", p=P)
-            if not last:
-                nc.vector.quantize_mx(out=codes[:].bitcast(FP8X4), scales=scl[:], in_=g[:])
-            for h in (1, 0):
-                if last:
-                    c = slice(h * 2 * P, (h + 1) * 2 * P)
-                    nc.vector.quantize_mx(
-                        out=codes[:, c].bitcast(FP8X4), scales=scl[:, c],
-                        in_=g[:, h * 2 * P * PACK : (h + 1) * 2 * P * PACK],
-                    )
-                acc = ps_out.tile([P, 2, D], F32, name="acc")
-                for j in range(2):
-                    c = slice((2 * h + j) * P, (2 * h + j + 1) * P)
-                    nc.tensor.matmul_mx(
-                        out=acc[:, j, :],
-                        lhsT=codes[:, c].bitcast(FP8X4), lhsT_scale=scl[:, c],
-                        rhs=kc[:].bitcast(FP8X4), rhs_scale=ks[:],
-                        start=True, stop=True,
-                    )
-                for j in range(2):
-                    i = 2 * h + j
-                    if last and j == 1:
-                        nc.vector.tensor_scalar_mul(out=res[:, i, :], in0=acc[:, j, :], scalar1=s["fac"][:, i : i + 1])
-                    else:
-                        nc.scalar.activation(
-                            out=res[:, i, :], in_=acc[:, j, :], func=ACT.Copy, scale=s["fac"][:, i : i + 1]
-                        )
-                if last:
-                    nc.sync.dma_start(out=dst[:, 2 * h : 2 * h + 2, :], in_=res[:, 2 * h : 2 * h + 2, :])
-            if not last:
-                nc.sync.dma_start(out=dst, in_=res[:])
+            other = "vector" if last else "scalar"
+            codes = work.tile([P, 2 * P], U32, name="wc", align_bytes=64)
+            scales = work.tile([P, 2 * P], U8, name="ws", align_bytes=64)
+            nc.vector.quantize_mx(out=codes[:].bitcast(FP8X4), scales=scales[:], in_=s["grouped"][:])
+            if b % 2:
+                codesb = work.tile([P, P], U32, name="wcb", bufs=2, align_bytes=64)
+                scalesb = work.tile([P, P], U8, name="wsb", bufs=2, align_bytes=64)
+                nc.vector.quantize_mx(out=codesb[:].bitcast(FP8X4), scales=scalesb[:], in_=s["groupedb"][:])
+
+            def mx(dst, lhs, lhs_s, rhs, rhs_s):
+                nc.tensor.matmul_mx(
+                    out=dst, lhsT=lhs.bitcast(FP8X4), lhsT_scale=lhs_s, rhs=rhs.bitcast(FP8X4), rhs_scale=rhs_s,
+                    start=True, stop=True,
+                )
+
+            acc3 = ps_out.tile([P, 2, D], F32, name="acc")
+            mx(acc3[:, 0, :], codes[:, 0:P], scales[:, 0:P], kc[b][:], ks[:, b, :])
+            j = b % N_KA
+            acc2 = ps_out.tile([P, 2, D], F32, name="acc")
+            mx(
+                acc2[:].rearrange("p h d -> p (h d)"), codes[:, P : 2 * P], scales[:, P : 2 * P],
+                ka[j][:].rearrange("p h d -> p (h d)"), ka_s[j][:].rearrange("p h d -> p (h d)"),
+            )
+            scale_out(b, 3, acc3[:, 0, :], "scalar")
+            scale_out(b, 2, acc2[:, 0, :], other)
+            store(b, 2)
+            scale_out(b, 0, acc2[:, 1, :], other)
+            if b % 2:
+                m = (b // 2) % N_KB
+                acc1 = ps_out.tile([P, 2, D], F32, name="acc")
+                mx(
+                    acc1[:].rearrange("p h d -> p (h d)"), codesb[:], scalesb[:],
+                    kb[m][:].rearrange("p h d -> p (h d)"), kb_s[m][:].rearrange("p h d -> p (h d)"),
+                )
+                scale_out(b - 1, 1, acc1[:, 0, :], "scalar")
+                store(b - 1, 0)
+                scale_out(b, 1, acc1[:, 1, :], "scalar")
+                store(b, 0)
 
         for i in ALL:
             row_sums(0, [i])
-            scales(0, [i])
-            mask_and_abs(0, [i])
+            mask(0, [i])
             spread(0, [i])
-            weights(0, i)
-            count(0, i)
+            multiply(0, i)
+            largest(0, i)
+        round_and_turn(0)
         factor(0)
         for b in range(K_ON_VECTOR):
             prepare_k(b)
         for b in range(1, B + 2):
             if b < B:
                 row_sums(b, ALL)
-                scales(b, ALL)
-                mask_and_abs(b, ALL)
+                mask(b, ALL)
                 spread(b, ALL)
                 if b >= K_ON_VECTOR:
                     prepare_k(b)
             if 1 <= b - 1 < B:
                 for i in reversed(ALL):
-                    weights(b - 1, i)
+                    multiply(b - 1, i)
+                round_and_turn(b - 1)
                 for i in reversed(ALL):
-                    count(b - 1, i)
+                    largest(b - 1, i)
                 factor(b - 1)
             if b - 2 >= 0:
                 product(b - 2)

@@ -25,7 +25,7 @@ REL_THRESH = 1e-09
 FLOPS = 2 * B * T * T * D
 
 DIAG_STEP = T + P
-K_ON_VECTOR = 2
+AHEAD = 4
 N_KA = 3
 N_KB = 2
 W_FIRST = {3: 0, 2: 512, 0: 896, 1: 1024}
@@ -61,37 +61,35 @@ def tile_symbolicpenaltytracker_kernel(tc, A_rel, k_seq, out):
             nc.sync.dma_start(out=k_sb[b][:], in_=k_seq[b].rearrange("(p u) d -> p u d", u=PACK))
 
         load_a(0)
-        for b in range(K_ON_VECTOR):
-            load_k(b)
-        for b in range(1, B):
+        for b in range(1, AHEAD):
             load_a(b)
-            if b >= K_ON_VECTOR:
-                load_k(b)
+            load_k(b - 1)
+        load_k(AHEAD - 1)
 
         warm = const.tile([P, 1], F32, name="warm")
         nc.vector.memset(warm[:], 1.0)
         nc.scalar.activation(out=warm[:], in_=warm[:], func=ACT.Sqrt)
 
-        tril_f = const.tile([P, P], F32, name="tril_f")
-        nc.gpsimd.memset(tril_f[:], 1.0)
+        tril = const.tile([P, P], BF16, name="tril")
+        nc.gpsimd.memset(tril[:], 1.0)
         nc.gpsimd.affine_select(
-            out=tril_f[:], in_=tril_f[:], compare_op=ALU.is_ge, fill=0.0, base=0,
+            out=tril[:], in_=tril[:], compare_op=ALU.is_ge, fill=0.0, base=0,
             pattern=[[-1, P]], channel_multiplier=1,
         )
         ident_f = const.tile([P, P], F32, name="ident_f")
         make_identity(nc, ident_f[:])
-        tril = const.tile([P, P], BF16, name="tril")
-        nc.vector.tensor_copy(out=tril[:], in_=tril_f[:])
 
         kc = [const.tile([P, D], U32, name="kc%d" % b, align_bytes=64) for b in range(B)]
-        ks = const.tile([P, B, D], U8, name="ks", align_bytes=64)
-        nc.vector.memset(ks[:].rearrange("p b d -> p (b d)").bitcast(I32), 0)
-        ka = [const.tile([P, 2, D], U32, name="ka%d" % j, align_bytes=64) for j in range(N_KA)]
-        ka_s = [const.tile([P, 2, D], U8, name="ka_s%d" % j, align_bytes=64) for j in range(N_KA)]
-        kb = [const.tile([P, 2, D], U32, name="kb%d" % j, align_bytes=64) for j in range(N_KB)]
-        kb_s = [const.tile([P, 2, D], U8, name="kb_s%d" % j, align_bytes=64) for j in range(N_KB)]
-        for t in ka + kb + ka_s + kb_s:
-            nc.vector.memset(t[:].rearrange("p h d -> p (h d)").bitcast(I32), 0)
+        kz = const.tile([P, N_KA + N_KB, 2, D], U32, name="kz", align_bytes=64)
+        planes = const.tile([P, 2 * (N_KA + N_KB) + B, D], U8, name="planes", align_bytes=64)
+        nc.vector.memset(kz[:, 0:N_KA, :, :].rearrange("p j h d -> p (j h d)").bitcast(I32), 0)
+        nc.gpsimd.memset(planes[:].rearrange("p b d -> p (b d)").bitcast(I32), 0)
+        nc.gpsimd.memset(kz[:, N_KA:, :, :].rearrange("p j h d -> p (j h d)").bitcast(I32), 0)
+        ka = [kz[:, j, :, :] for j in range(N_KA)]
+        kb = [kz[:, N_KA + j, :, :] for j in range(N_KB)]
+        ka_s = [planes[:, 2 * j : 2 * j + 2, :] for j in range(N_KA)]
+        kb_s = [planes[:, 2 * (N_KA + j) : 2 * (N_KA + j) + 2, :] for j in range(N_KB)]
+        ks = planes[:, 2 * (N_KA + N_KB) :, :]
 
         state = [{} for b in range(B)]
         ALL = list(range(NB))
@@ -101,21 +99,19 @@ def tile_symbolicpenaltytracker_kernel(tc, A_rel, k_seq, out):
                 state[b][name] = make()
             return state[b][name]
 
-        def prepare_k(b):
+        def regroup_k(b):
             kg = work.tile([P, D * PACK], BF16, name="kg", align_bytes=64)
-            if b < K_ON_VECTOR:
-                nc.vector.tensor_copy(
-                    out=kg[:].rearrange("p (c i u) -> p c u i", i=4, u=PACK),
-                    in_=k_sb[b][:].rearrange("p u (c i) -> p c u i", i=4),
-                )
-            else:
-                nc.gpsimd.tensor_scalar(
-                    out=kg[:].rearrange("p (d u) -> p d u", u=PACK),
-                    in0=k_sb[b][:].rearrange("p u d -> p d u"),
-                    scalar1=1.0, scalar2=0.0, op0=ALU.mult, op1=ALU.add,
-                )
-            nc.vector.quantize_mx(out=kc[b][:].bitcast(FP8X4), scales=ks[:, b, :], in_=kg[:])
+            state[b]["kg"] = kg
+            nc.gpsimd.tensor_scalar(
+                out=kg[:].rearrange("p (d u) -> p d u", u=PACK),
+                in0=k_sb[b][:].rearrange("p u d -> p d u"),
+                scalar1=1.0, scalar2=0.0, op0=ALU.mult, op1=ALU.add,
+            )
 
+        def quantise_k(b):
+            nc.vector.quantize_mx(out=kc[b][:].bitcast(FP8X4), scales=ks[:, b, :], in_=state[b]["kg"][:])
+
+        def move_k(b):
             def move(dst, dst_s, half, p0, n):
                 nc.sync.dma_start(
                     out=dst[p0 : p0 + n, half, :].bitcast(I32), in_=kc[b][0:n, :].bitcast(I32)
@@ -130,18 +126,27 @@ def tile_symbolicpenaltytracker_kernel(tc, A_rel, k_seq, out):
             m = (b // 2) % N_KB
             move(kb[m], kb_s[m], b % 2, (b % 2) * 2 * Q, 2 * Q)
 
-        def row_sums(b, blocks):
+        def row_sum(b, i, engine):
             deg = tile_of(b, "deg", lambda: small.tile([P, NB], F32, name="deg"))
-            sd = tile_of(b, "sd", lambda: small.tile([P, NB], F32, name="sd"))
-            dis = tile_of(b, "dis", lambda: small.tile([P, NB], F32, name="dis"))
-            for i in blocks:
-                unused = work.tile([P, T], BF16, name="unused")
+            if engine == "vector":
+                unused = work.tile([P, T], BF16, name="unused_v")
+                nc.vector.tensor_scalar(
+                    out=unused[:], in0=rows(b)[:, i, :], scalar1=1.0, scalar2=None,
+                    op0=ALU.mult, op1=ALU.add, accum_out=deg[:, i : i + 1],
+                )
+            else:
+                unused = work.tile([P, T], BF16, name="unused_s")
                 nc.scalar.activation(
                     out=unused[:], in_=rows(b)[:, i, :], func=ACT.Copy, accum_out=deg[:, i : i + 1]
                 )
-            c = slice(blocks[0], blocks[-1] + 1)
-            nc.scalar.activation(out=sd[:, c], in_=deg[:, c], func=ACT.Sqrt, bias=EPS)
-            nc.vector.reciprocal(out=dis[:, c], in_=sd[:, c])
+
+        def root(b, c):
+            sd = tile_of(b, "sd", lambda: small.tile([P, NB], F32, name="sd"))
+            nc.scalar.activation(out=sd[:, c], in_=state[b]["deg"][:, c], func=ACT.Sqrt, bias=EPS)
+
+        def invert(b, c):
+            dis = tile_of(b, "dis", lambda: small.tile([P, NB], F32, name="dis"))
+            nc.vector.reciprocal(out=dis[:, c], in_=state[b]["sd"][:, c])
 
         def spread(b, blocks):
             dis_all = tile_of(b, "dis_all", lambda: ps_dis.tile([P, T], F32, name="dis_all"))
@@ -174,37 +179,53 @@ def tile_symbolicpenaltytracker_kernel(tc, A_rel, k_seq, out):
                 in1=state[b]["dis_all"][:, 0:n], op0=ALU.mult, op1=ALU.mult,
             )
 
-        def round_and_turn(b):
-            s = state[b]
-            w16 = work.tile([P, W_MAIN], BF16, name="w16", align_bytes=64)
-            nc.vector.tensor_copy(out=w16[:], in_=s["w32"][:, 0:W_MAIN])
-            even = b - b % 2
-            w16b = tile_of(even, "w16b", lambda: work.tile([P, 2, 2 * P], BF16, name="w16b", bufs=2, align_bytes=64))
-            nc.vector.tensor_copy(out=w16b[:, b % 2, :], in_=s["w32"][:, W_MAIN:W_ALL])
+        def round_main(b, tiles):
+            w16 = tile_of(b, "w16", lambda: work.tile([P, W_MAIN], BF16, name="w16", align_bytes=64))
+            c = slice(tiles[0] * T, (tiles[-1] + 1) * T)
+            nc.vector.tensor_copy(out=w16[:, c], in_=state[b]["w32"][:, c])
+
+        def round_shared(b):
+            w16b = tile_of(
+                b - b % 2, "w16b", lambda: work.tile([P, 2, 2 * P], BF16, name="w16b", bufs=2, align_bytes=64)
+            )
+            nc.vector.tensor_copy(out=w16b[:, b % 2, :], in_=state[b]["w32"][:, W_MAIN:W_ALL])
+
+        def turn_main(b, tiles):
             wt = ps_wt.tile([P, 2, 2, P], F32, name="wt", bufs=2)
-            words = w16[:].bitcast(F32)
-            for j in range(2):
+            state[b]["wt", tiles] = wt
+            words = state[b]["w16"][:].bitcast(F32)
+            for j in tiles:
                 for v in range(2):
                     nc.tensor.transpose(
                         out=wt[:, j, v, :], in_=words[:, j * 256 + v : (j + 1) * 256 : 2], identity=ident_f[:]
                     )
-            grouped = work.tile([P, 2 * P * PACK], BF16, name="grouped", align_bytes=64)
-            s["grouped"] = grouped
-            nc.scalar.copy(
-                out=grouped[:].bitcast(F32).rearrange("p (j t v) -> p j t v", t=P, v=2),
-                in_=wt[:].rearrange("p j v t -> p j t v"),
+
+        def copy_main(b, tiles):
+            grouped = tile_of(
+                b, "grouped", lambda: work.tile([P, 2, P * PACK], BF16, name="grouped", align_bytes=64)
             )
-            if b % 2:
-                wtb = ps_wt.tile([P, 2, P], F32, name="wtb")
-                words = w16b[:].rearrange("p h s -> p (h s)").bitcast(F32)
-                for v in range(2):
-                    nc.tensor.transpose(out=wtb[:, v, :], in_=words[:, v::2], identity=ident_f[:])
-                groupedb = work.tile([P, P * PACK], BF16, name="groupedb", bufs=2, align_bytes=64)
-                s["groupedb"] = groupedb
-                nc.scalar.copy(
-                    out=groupedb[:].bitcast(F32).rearrange("p (t v) -> p t v", v=2),
-                    in_=wtb[:].rearrange("p v t -> p t v"),
-                )
+            wt = state[b]["wt", tiles]
+            c = slice(tiles[0], tiles[-1] + 1)
+            nc.scalar.copy(
+                out=grouped[:, c, :].bitcast(F32).rearrange("p j (t v) -> p j t v", v=2),
+                in_=wt[:, c, :, :].rearrange("p j v t -> p j t v"),
+            )
+
+        def turn_shared(b):
+            wtb = ps_wt.tile([P, 2, P], F32, name="wtb")
+            words = state[b - 1]["w16b"][:].rearrange("p h s -> p (h s)").bitcast(F32)
+            for v in range(2):
+                nc.tensor.transpose(out=wtb[:, v, :], in_=words[:, v::2], identity=ident_f[:])
+            state[b]["wtb"] = wtb
+
+        def copy_shared(b):
+            wtb = state[b]["wtb"]
+            groupedb = work.tile([P, P * PACK], BF16, name="groupedb", bufs=2, align_bytes=64)
+            state[b]["groupedb"] = groupedb
+            nc.scalar.copy(
+                out=groupedb[:].bitcast(F32).rearrange("p (t v) -> p t v", v=2),
+                in_=wtb[:].rearrange("p v t -> p t v"),
+            )
 
         def largest(b, i):
             top = tile_of(b, "top", lambda: small.tile([P, NB], F32, name="top"))
@@ -212,11 +233,12 @@ def tile_symbolicpenaltytracker_kernel(tc, A_rel, k_seq, out):
                 out=top[:, i : i + 1], in_=w32(b, i), axis=AX.X, op=ALU.max, apply_absolute_value=True
             )
 
-        def factor(b):
+        def factor(b, blocks):
             fac = tile_of(b, "fac", lambda: small.tile([P, NB], F32, name="fac"))
             engine = nc.vector if b == B - 1 else nc.gpsimd
+            c = slice(blocks[0], blocks[-1] + 1)
             engine.tensor_scalar(
-                out=fac[:], in0=state[b]["top"][:], scalar1=REL_THRESH, scalar2=math.sqrt(GAMMA),
+                out=fac[:, c], in0=state[b]["top"][:, c], scalar1=REL_THRESH, scalar2=math.sqrt(GAMMA),
                 op0=ALU.is_gt, op1=ALU.mult,
             )
 
@@ -228,75 +250,186 @@ def tile_symbolicpenaltytracker_kernel(tc, A_rel, k_seq, out):
             else:
                 nc.vector.tensor_scalar_mul(out=res[:, i, :], in0=acc, scalar1=fac)
 
-        def store(b, i0):
+        def store(b, i0, n):
             dst = out[b].rearrange("(i p) d -> p i d", p=P)
-            nc.sync.dma_start(out=dst[:, i0 : i0 + 2, :], in_=state[b]["res"][:, i0 : i0 + 2, :])
+            nc.sync.dma_start(out=dst[:, i0 : i0 + n, :], in_=state[b]["res"][:, i0 : i0 + n, :])
 
-        def product(b):
-            s = state[b]
-            last = b == B - 1
-            other = "vector" if last else "scalar"
-            codes = work.tile([P, 2 * P], U32, name="wc", align_bytes=64)
-            scales = work.tile([P, 2 * P], U8, name="ws", align_bytes=64)
-            nc.vector.quantize_mx(out=codes[:].bitcast(FP8X4), scales=scales[:], in_=s["grouped"][:])
-            if b % 2:
-                codesb = work.tile([P, P], U32, name="wcb", bufs=2, align_bytes=64)
-                scalesb = work.tile([P, P], U8, name="wsb", bufs=2, align_bytes=64)
-                nc.vector.quantize_mx(out=codesb[:].bitcast(FP8X4), scales=scalesb[:], in_=s["groupedb"][:])
-
-            def mx(dst, lhs, lhs_s, rhs, rhs_s):
-                nc.tensor.matmul_mx(
-                    out=dst, lhsT=lhs.bitcast(FP8X4), lhsT_scale=lhs_s, rhs=rhs.bitcast(FP8X4), rhs_scale=rhs_s,
-                    start=True, stop=True,
-                )
-
-            acc3 = ps_out.tile([P, 2, D], F32, name="acc")
-            mx(acc3[:, 0, :], codes[:, 0:P], scales[:, 0:P], kc[b][:], ks[:, b, :])
-            j = b % N_KA
-            acc2 = ps_out.tile([P, 2, D], F32, name="acc")
-            mx(
-                acc2[:].rearrange("p h d -> p (h d)"), codes[:, P : 2 * P], scales[:, P : 2 * P],
-                ka[j][:].rearrange("p h d -> p (h d)"), ka_s[j][:].rearrange("p h d -> p (h d)"),
+        def mx(dst, lhs, lhs_s, rhs, rhs_s):
+            nc.tensor.matmul_mx(
+                out=dst, lhsT=lhs.bitcast(FP8X4), lhsT_scale=lhs_s, rhs=rhs.bitcast(FP8X4), rhs_scale=rhs_s,
+                start=True, stop=True,
             )
-            scale_out(b, 3, acc3[:, 0, :], "scalar")
-            scale_out(b, 2, acc2[:, 0, :], other)
-            store(b, 2)
-            scale_out(b, 0, acc2[:, 1, :], other)
+
+        def quantise_main(b, tiles):
+            codes = tile_of(b, "wc", lambda: work.tile([P, 2 * P], U32, name="wc", align_bytes=64))
+            scales = tile_of(b, "ws", lambda: work.tile([P, 2 * P], U8, name="ws", align_bytes=64))
+            c = slice(tiles[0] * P, (tiles[-1] + 1) * P)
+            nc.vector.quantize_mx(
+                out=codes[:, c].bitcast(FP8X4), scales=scales[:, c],
+                in_=state[b]["grouped"][:].rearrange("p j x -> p (j x)")[:, c.start * PACK : c.stop * PACK],
+            )
+
+        def quantise_shared(b):
+            s = state[b]
+            s["wcb"] = work.tile([P, P], U32, name="wcb", bufs=2, align_bytes=64)
+            s["wsb"] = work.tile([P, P], U8, name="wsb", bufs=2, align_bytes=64)
+            nc.vector.quantize_mx(out=s["wcb"][:].bitcast(FP8X4), scales=s["wsb"][:], in_=s["groupedb"][:])
+
+        def product_3(b):
+            s = state[b]
+            s["acc3"] = ps_out.tile([P, 2, D], F32, name="acc")
+            mx(s["acc3"][:, 0, :], s["wc"][:, 0:P], s["ws"][:, 0:P], kc[b][:], ks[:, b, :])
+
+        def product_20(b):
+            s = state[b]
+            s["acc20"] = ps_out.tile([P, 2, D], F32, name="acc")
+            j = b % N_KA
+            mx(
+                s["acc20"][:].rearrange("p h d -> p (h d)"), s["wc"][:, P : 2 * P], s["ws"][:, P : 2 * P],
+                ka[j].rearrange("p h d -> p (h d)"), ka_s[j].rearrange("p h d -> p (h d)"),
+            )
+
+        def product_shared(b):
+            s = state[b]
+            s["acc1"] = ps_out.tile([P, 2, D], F32, name="acc")
+            m = (b // 2) % N_KB
+            mx(
+                s["acc1"][:].rearrange("p h d -> p (h d)"), s["wcb"][:], s["wsb"][:],
+                kb[m].rearrange("p h d -> p (h d)"), kb_s[m].rearrange("p h d -> p (h d)"),
+            )
+
+        def quantise_w(b):
+            quantise_main(b, (0, 1))
             if b % 2:
-                m = (b // 2) % N_KB
-                acc1 = ps_out.tile([P, 2, D], F32, name="acc")
-                mx(
-                    acc1[:].rearrange("p h d -> p (h d)"), codesb[:], scalesb[:],
-                    kb[m][:].rearrange("p h d -> p (h d)"), kb_s[m][:].rearrange("p h d -> p (h d)"),
-                )
-                scale_out(b - 1, 1, acc1[:, 0, :], "scalar")
-                store(b - 1, 0)
-                scale_out(b, 1, acc1[:, 1, :], "scalar")
-                store(b, 0)
+                quantise_shared(b)
+
+        def products(b):
+            product_3(b)
+            product_20(b)
+            if b % 2:
+                product_shared(b)
+
+        def outputs(b):
+            s = state[b]
+            scale_out(b, 3, s["acc3"][:, 0, :], "scalar")
+            scale_out(b, 2, s["acc20"][:, 0, :], "scalar")
+            store(b, 2, 2)
+            scale_out(b, 0, s["acc20"][:, 1, :], "scalar")
+            if b % 2:
+                scale_out(b - 1, 1, s["acc1"][:, 0, :], "scalar")
+                store(b - 1, 0, 2)
+                scale_out(b, 1, s["acc1"][:, 1, :], "scalar")
+                store(b, 0, 2)
+
+        ctx.enter_context(tc.manual_schedule())
+        EVERY = slice(0, NB)
+        LO = slice(0, 2)
+        HI = slice(2, 4)
 
         for i in ALL:
-            row_sums(0, [i])
-            mask(0, [i])
-            spread(0, [i])
-            multiply(0, i)
-            largest(0, i)
-        round_and_turn(0)
-        factor(0)
-        for b in range(K_ON_VECTOR):
-            prepare_k(b)
-        for b in range(1, B + 2):
-            if b < B:
-                row_sums(b, ALL)
-                mask(b, ALL)
-                spread(b, ALL)
-                if b >= K_ON_VECTOR:
-                    prepare_k(b)
-            if 1 <= b - 1 < B:
-                for i in reversed(ALL):
-                    multiply(b - 1, i)
-                round_and_turn(b - 1)
-                for i in reversed(ALL):
-                    largest(b - 1, i)
-                factor(b - 1)
-            if b - 2 >= 0:
-                product(b - 2)
+            row_sum(0, i, ("scalar", "vector")[i % 2])
+            if i == 1:
+                root(0, LO)
+        root(0, HI)
+        mask(0, [1])
+        mask(0, [3])
+        invert(0, LO)
+        spread(0, [0, 1])
+        mask(0, [0])
+        multiply(0, 0)
+        multiply(0, 1)
+        invert(0, HI)
+        spread(0, [2, 3])
+        mask(0, [2])
+        multiply(0, 2)
+        multiply(0, 3)
+        for i in ALL:
+            row_sum(1, i, "scalar")
+        root(1, EVERY)
+        regroup_k(0)
+        regroup_k(1)
+        for n in range(B - 1):
+            if n + AHEAD < B:
+                load_a(n + AHEAD)
+                load_k(n + AHEAD)
+            if n + 2 < B:
+                regroup_k(n + 2)
+            if n > 0:
+                invert(n + 1, EVERY)
+                spread(n + 1, ALL)
+                for i in (3, 2, 0, 1):
+                    multiply(n, i)
+                quantise_w(n - 1)
+                products(n - 1)
+            if n + 2 < B:
+                for i in ALL:
+                    row_sum(n + 2, i, "scalar")
+                root(n + 2, EVERY)
+            if n > 0:
+                quantise_k(n)
+                move_k(n)
+            round_main(n, (0, 1))
+            round_shared(n)
+            if n == 0:
+                quantise_k(0)
+                move_k(0)
+            turn_main(n, (0, 1))
+            if n % 2:
+                turn_shared(n)
+            if n > 0:
+                outputs(n - 1)
+            copy_main(n, (0, 1))
+            if n % 2:
+                copy_shared(n)
+            largest(n, 3)
+            largest(n, 2)
+            if n == 0:
+                invert(1, EVERY)
+                spread(1, ALL)
+            mask(n + 1, ALL)
+            largest(n, 0)
+            largest(n, 1)
+            factor(n, ALL)
+        z = B - 1
+        quantise_k(z)
+        move_k(z)
+        multiply(z, 1)
+        multiply(z, 3)
+        round_shared(z)
+        turn_shared(z)
+        quantise_w(z - 1)
+        products(z - 1)
+        round_main(z, (0,))
+        turn_main(z, (0,))
+        copy_shared(z)
+        outputs(z - 1)
+        multiply(z, 2)
+        multiply(z, 0)
+        copy_main(z, (0,))
+        largest(z, 1)
+        round_main(z, (1,))
+        turn_main(z, (1,))
+        quantise_shared(z)
+        product_shared(z)
+        largest(z, 3)
+        quantise_main(z, (0,))
+        product_3(z)
+        factor(z, [1])
+        factor(z, [3])
+        copy_main(z, (1,))
+        scale_out(z - 1, 1, state[z]["acc1"][:, 0, :], "scalar")
+        store(z - 1, 0, 2)
+        largest(z, 2)
+        largest(z, 0)
+        quantise_main(z, (1,))
+        product_20(z)
+        factor(z, [2])
+        factor(z, [0])
+        scale_out(z, 1, state[z]["acc1"][:, 1, :], "vector")
+        store(z, 1, 1)
+        scale_out(z, 3, state[z]["acc3"][:, 0, :], "scalar")
+        store(z, 3, 1)
+        scale_out(z, 2, state[z]["acc20"][:, 0, :], "scalar")
+        store(z, 2, 1)
+        scale_out(z, 0, state[z]["acc20"][:, 1, :], "vector")
+        store(z, 0, 1)

@@ -25,12 +25,11 @@ REL_THRESH = 1e-09
 FLOPS = 2 * B * T * T * D
 
 DIAG_STEP = T + P
+SUMS_ON_VECTOR = (0,)
 AHEAD = 4
 N_KA = 3
 N_KB = 2
-W_FIRST = {3: 0, 2: 512, 0: 896, 1: 1024}
-W_MAIN = 1024
-W_ALL = 1280
+W_FIRST = {3: 0, 2: 512, 0: 896}
 
 
 def tile_symbolicpenaltytracker_kernel(tc, A_rel, k_seq, out):
@@ -41,7 +40,7 @@ def tile_symbolicpenaltytracker_kernel(tc, A_rel, k_seq, out):
         small = ctx.enter_context(tc.tile_pool(name="small", bufs=4))
         work = ctx.enter_context(tc.tile_pool(name="work", bufs=3))
         ps_dis = ctx.enter_context(tc.psum_pool(name="ps_dis", bufs=2))
-        ps_wt = ctx.enter_context(tc.psum_pool(name="ps_wt", bufs=1))
+        ps_wt = ctx.enter_context(tc.psum_pool(name="ps_wt", bufs=3))
         ps_out = ctx.enter_context(tc.psum_pool(name="ps_out", bufs=3))
 
         a_sb = [resid.tile([P, NB * DIAG_STEP], BF16, name="a%d" % b) for b in range(B)]
@@ -169,62 +168,41 @@ def tile_symbolicpenaltytracker_kernel(tc, A_rel, k_seq, out):
                 )
 
         def w32(b, i):
-            return state[b]["w32"][:, W_FIRST[i] : W_FIRST[i] + (i + 1) * P]
+            if i == 1:
+                shared = tile_of(b - b % 2, "w32b", lambda: work.tile([P, 2, 2 * P], F32, name="w32b", bufs=2))
+                return shared[:, b % 2, :]
+            main = tile_of(b, "w32", lambda: work.tile([P, 2 * T], F32, name="w32"))
+            return main[:, W_FIRST[i] : W_FIRST[i] + (i + 1) * P]
 
         def multiply(b, i):
-            tile_of(b, "w32", lambda: work.tile([P, W_ALL], F32, name="w32"))
             n = (i + 1) * P
             nc.vector.scalar_tensor_tensor(
                 out=w32(b, i), in0=rows(b)[:, i, 0:n], scalar=state[b]["dis"][:, i : i + 1],
                 in1=state[b]["dis_all"][:, 0:n], op0=ALU.mult, op1=ALU.mult,
             )
 
-        def round_main(b, tiles):
-            w16 = tile_of(b, "w16", lambda: work.tile([P, W_MAIN], BF16, name="w16", align_bytes=64))
-            c = slice(tiles[0] * T, (tiles[-1] + 1) * T)
-            nc.vector.tensor_copy(out=w16[:, c], in_=state[b]["w32"][:, c])
+        def turn(b, tile):
+            wt = ps_wt.tile([P, PACK, P], F32, name="wt")
+            state[b]["wt", tile] = wt
+            if tile == "shared":
+                w = state[b - 1]["w32b"][:].rearrange("p h s -> p (h s)")
+            else:
+                w = state[b]["w32"][:, tile * T : (tile + 1) * T]
+            for u in range(PACK):
+                nc.tensor.transpose(out=wt[:, u, :], in_=w[:, u::PACK], identity=ident_f[:])
 
-        def round_shared(b):
-            w16b = tile_of(
-                b - b % 2, "w16b", lambda: work.tile([P, 2, 2 * P], BF16, name="w16b", bufs=2, align_bytes=64)
-            )
-            nc.vector.tensor_copy(out=w16b[:, b % 2, :], in_=state[b]["w32"][:, W_MAIN:W_ALL])
-
-        def turn_main(b, tiles):
-            wt = ps_wt.tile([P, 2, 2, P], F32, name="wt", bufs=2)
-            state[b]["wt", tiles] = wt
-            words = state[b]["w16"][:].bitcast(F32)
-            for j in tiles:
-                for v in range(2):
-                    nc.tensor.transpose(
-                        out=wt[:, j, v, :], in_=words[:, j * 256 + v : (j + 1) * 256 : 2], identity=ident_f[:]
-                    )
-
-        def copy_main(b, tiles):
-            grouped = tile_of(
-                b, "grouped", lambda: work.tile([P, 2, P * PACK], BF16, name="grouped", align_bytes=64)
-            )
-            wt = state[b]["wt", tiles]
-            c = slice(tiles[0], tiles[-1] + 1)
+        def copy_w(b, tile):
+            if tile == "shared":
+                state[b]["groupedb"] = work.tile([P, P * PACK], BF16, name="groupedb", bufs=2, align_bytes=64)
+                dst = state[b]["groupedb"][:]
+            else:
+                grouped = tile_of(
+                    b, "grouped", lambda: work.tile([P, 2, P * PACK], BF16, name="grouped", align_bytes=64)
+                )
+                dst = grouped[:, tile, :]
             nc.scalar.copy(
-                out=grouped[:, c, :].bitcast(F32).rearrange("p j (t v) -> p j t v", v=2),
-                in_=wt[:, c, :, :].rearrange("p j v t -> p j t v"),
-            )
-
-        def turn_shared(b):
-            wtb = ps_wt.tile([P, 2, P], F32, name="wtb")
-            words = state[b - 1]["w16b"][:].rearrange("p h s -> p (h s)").bitcast(F32)
-            for v in range(2):
-                nc.tensor.transpose(out=wtb[:, v, :], in_=words[:, v::2], identity=ident_f[:])
-            state[b]["wtb"] = wtb
-
-        def copy_shared(b):
-            wtb = state[b]["wtb"]
-            groupedb = work.tile([P, P * PACK], BF16, name="groupedb", bufs=2, align_bytes=64)
-            state[b]["groupedb"] = groupedb
-            nc.scalar.copy(
-                out=groupedb[:].bitcast(F32).rearrange("p (t v) -> p t v", v=2),
-                in_=wtb[:].rearrange("p v t -> p t v"),
+                out=dst.rearrange("p (t u) -> p t u", u=PACK),
+                in_=state[b]["wt", tile][:].rearrange("p u t -> p t u"),
             )
 
         def largest(b, i):
@@ -359,28 +337,33 @@ def tile_symbolicpenaltytracker_kernel(tc, A_rel, k_seq, out):
                 spread(n + 1, ALL)
                 for i in (3, 2, 0, 1):
                     multiply(n, i)
+            turn(n, 0)
+            turn(n, 1)
+            if n % 2:
+                turn(n, "shared")
+            if n > 0:
                 quantise_w(n - 1)
                 products(n - 1)
             if n + 2 < B:
                 for i in ALL:
-                    row_sum(n + 2, i, "scalar")
-                root(n + 2, EVERY)
+                    row_sum(n + 2, i, "vector" if i in SUMS_ON_VECTOR else "scalar")
             if n > 0:
                 quantise_k(n)
                 move_k(n)
-            round_main(n, (0, 1))
-            round_shared(n)
+            if n == B - 2:
+                quantise_k(B - 1)
+                move_k(B - 1)
+            copy_w(n, 0)
+            copy_w(n, 1)
+            if n + 2 < B:
+                root(n + 2, EVERY)
+            if n % 2:
+                copy_w(n, "shared")
+            if n > 0:
+                outputs(n - 1)
             if n == 0:
                 quantise_k(0)
                 move_k(0)
-            turn_main(n, (0, 1))
-            if n % 2:
-                turn_shared(n)
-            if n > 0:
-                outputs(n - 1)
-            copy_main(n, (0, 1))
-            if n % 2:
-                copy_shared(n)
             largest(n, 3)
             largest(n, 2)
             if n == 0:
@@ -391,24 +374,19 @@ def tile_symbolicpenaltytracker_kernel(tc, A_rel, k_seq, out):
             largest(n, 1)
             factor(n, ALL)
         z = B - 1
-        quantise_k(z)
-        move_k(z)
         multiply(z, 1)
+        turn(z, "shared")
         multiply(z, 3)
-        round_shared(z)
-        turn_shared(z)
+        turn(z, 0)
         quantise_w(z - 1)
         products(z - 1)
-        round_main(z, (0,))
-        turn_main(z, (0,))
-        copy_shared(z)
+        copy_w(z, "shared")
+        copy_w(z, 0)
         outputs(z - 1)
         multiply(z, 2)
         multiply(z, 0)
-        copy_main(z, (0,))
+        turn(z, 1)
         largest(z, 1)
-        round_main(z, (1,))
-        turn_main(z, (1,))
         quantise_shared(z)
         product_shared(z)
         largest(z, 3)
@@ -416,7 +394,7 @@ def tile_symbolicpenaltytracker_kernel(tc, A_rel, k_seq, out):
         product_3(z)
         factor(z, [1])
         factor(z, [3])
-        copy_main(z, (1,))
+        copy_w(z, 1)
         scale_out(z - 1, 1, state[z]["acc1"][:, 0, :], "scalar")
         store(z - 1, 0, 2)
         largest(z, 2)

@@ -29,7 +29,9 @@ SUMS_ON_VECTOR = (0,)
 AHEAD = 4
 N_KA = 3
 N_KB = 2
-W_FIRST = {3: 0, 2: 512, 0: 896}
+W_FIRST = ({3: 0, 2: 512, 0: 896, 1: 1024}, {1: 1280, 2: 1536, 0: 1920, 3: 2048})
+W_SHARED = 1024
+W_PAIR = 2560
 
 
 def tile_symbolicpenaltytracker_kernel(tc, A_rel, k_seq, out):
@@ -168,11 +170,9 @@ def tile_symbolicpenaltytracker_kernel(tc, A_rel, k_seq, out):
                 )
 
         def w32(b, i):
-            if i == 1:
-                shared = tile_of(b - b % 2, "w32b", lambda: work.tile([P, 2, 2 * P], F32, name="w32b", bufs=2))
-                return shared[:, b % 2, :]
-            main = tile_of(b, "w32", lambda: work.tile([P, 2 * T], F32, name="w32"))
-            return main[:, W_FIRST[i] : W_FIRST[i] + (i + 1) * P]
+            pair = tile_of(b - b % 2, "w32", lambda: work.tile([P, W_PAIR], F32, name="w32", bufs=2))
+            first = W_FIRST[b % 2][i]
+            return pair[:, first : first + (i + 1) * P]
 
         def multiply(b, i):
             n = (i + 1) * P
@@ -184,10 +184,8 @@ def tile_symbolicpenaltytracker_kernel(tc, A_rel, k_seq, out):
         def turn(b, tile):
             wt = ps_wt.tile([P, PACK, P], F32, name="wt")
             state[b]["wt", tile] = wt
-            if tile == "shared":
-                w = state[b - 1]["w32b"][:].rearrange("p h s -> p (h s)")
-            else:
-                w = state[b]["w32"][:, tile * T : (tile + 1) * T]
+            first = W_SHARED if tile == "shared" else W_FIRST[b % 2][(3, 2)[tile]]
+            w = state[b - b % 2]["w32"][:, first : first + T]
             for u in range(PACK):
                 nc.tensor.transpose(out=wt[:, u, :], in_=w[:, u::PACK], identity=ident_f[:])
 
@@ -211,18 +209,25 @@ def tile_symbolicpenaltytracker_kernel(tc, A_rel, k_seq, out):
                 out=top[:, i : i + 1], in_=w32(b, i), axis=AX.X, op=ALU.max, apply_absolute_value=True
             )
 
-        def factor(b, blocks):
-            fac = tile_of(b, "fac", lambda: small.tile([P, NB], F32, name="fac"))
-            engine = nc.vector if b == B - 1 else nc.gpsimd
-            c = slice(blocks[0], blocks[-1] + 1)
+        def largest_3(b):
+            largest(b, 3)
+
+        def largest_210(b):
+            for i in (2, 1, 0):
+                largest(b, i)
+
+        def factors(b):
+            fac = small.tile([P, NB], F32, name="fac")
+            engine = nc.gpsimd
             engine.tensor_scalar(
-                out=fac[:, c], in0=state[b]["top"][:, c], scalar1=REL_THRESH, scalar2=math.sqrt(GAMMA),
+                out=fac[:], in0=state[b]["top"][:], scalar1=REL_THRESH, scalar2=math.sqrt(GAMMA),
                 op0=ALU.is_gt, op1=ALU.mult,
             )
+            state[b]["fac"] = [fac[:, i : i + 1] for i in ALL]
 
         def scale_out(b, i, acc, engine):
             res = tile_of(b, "res", lambda: work.tile([P, NB, D], F32, name="res", bufs=4))
-            fac = state[b]["fac"][:, i : i + 1]
+            fac = state[b]["fac"][i]
             if engine == "scalar":
                 nc.scalar.activation(out=res[:, i, :], in_=acc, func=ACT.Copy, scale=fac)
             else:
@@ -326,7 +331,7 @@ def tile_symbolicpenaltytracker_kernel(tc, A_rel, k_seq, out):
         root(1, EVERY)
         regroup_k(0)
         regroup_k(1)
-        for n in range(B - 1):
+        for n in range(B - 2):
             if n + AHEAD < B:
                 load_a(n + AHEAD)
                 load_k(n + AHEAD)
@@ -341,73 +346,80 @@ def tile_symbolicpenaltytracker_kernel(tc, A_rel, k_seq, out):
             turn(n, 1)
             if n % 2:
                 turn(n, "shared")
-            if n > 0:
-                quantise_w(n - 1)
-                products(n - 1)
             if n + 2 < B:
                 for i in ALL:
                     row_sum(n + 2, i, "vector" if i in SUMS_ON_VECTOR else "scalar")
-            if n > 0:
-                quantise_k(n)
-                move_k(n)
-            if n == B - 2:
-                quantise_k(B - 1)
-                move_k(B - 1)
+                root(n + 2, EVERY)
+            if n > 1:
+                outputs(n - 2)
             copy_w(n, 0)
             copy_w(n, 1)
-            if n + 2 < B:
-                root(n + 2, EVERY)
             if n % 2:
                 copy_w(n, "shared")
-            if n > 0:
-                outputs(n - 1)
             if n == 0:
                 quantise_k(0)
                 move_k(0)
-            largest(n, 3)
-            largest(n, 2)
+            largest_3(n)
             if n == 0:
                 invert(1, EVERY)
                 spread(1, ALL)
             mask(n + 1, ALL)
-            largest(n, 0)
-            largest(n, 1)
-            factor(n, ALL)
+            largest_210(n)
+            factors(n)
+            if n > 0:
+                quantise_w(n - 1)
+                products(n - 1)
+            quantise_k(n + 1)
+            move_k(n + 1)
+        y = B - 2
         z = B - 1
+        invert(z, EVERY)
+        spread(z, ALL)
+        for i in (3, 2, 0, 1):
+            multiply(y, i)
+        turn(y, 0)
+        turn(y, 1)
+        outputs(y - 2)
+        copy_w(y, 0)
+        copy_w(y, 1)
+        quantise_k(z)
+        move_k(z)
+        mask(z, ALL)
+        quantise_w(y - 1)
+        products(y - 1)
+        outputs(y - 1)
         multiply(z, 1)
         turn(z, "shared")
         multiply(z, 3)
         turn(z, 0)
-        quantise_w(z - 1)
-        products(z - 1)
+        largest_3(y)
+        quantise_w(y)
+        products(y)
+        largest_210(y)
+        factors(y)
         copy_w(z, "shared")
         copy_w(z, 0)
-        outputs(z - 1)
         multiply(z, 2)
         multiply(z, 0)
         turn(z, 1)
-        largest(z, 1)
+        outputs(y)
+        copy_w(z, 1)
+        largest_210(z)
         quantise_shared(z)
         product_shared(z)
-        largest(z, 3)
+        largest_3(z)
+        factors(z)
         quantise_main(z, (0,))
         product_3(z)
-        factor(z, [1])
-        factor(z, [3])
-        copy_w(z, 1)
-        scale_out(z - 1, 1, state[z]["acc1"][:, 0, :], "scalar")
-        store(z - 1, 0, 2)
-        largest(z, 2)
-        largest(z, 0)
+        scale_out(y, 1, state[z]["acc1"][:, 0, :], "scalar")
+        store(y, 0, 2)
         quantise_main(z, (1,))
         product_20(z)
-        factor(z, [2])
-        factor(z, [0])
         scale_out(z, 1, state[z]["acc1"][:, 1, :], "vector")
         store(z, 1, 1)
         scale_out(z, 3, state[z]["acc3"][:, 0, :], "scalar")
         store(z, 3, 1)
-        scale_out(z, 2, state[z]["acc20"][:, 0, :], "scalar")
-        store(z, 2, 1)
         scale_out(z, 0, state[z]["acc20"][:, 1, :], "vector")
         store(z, 0, 1)
+        scale_out(z, 2, state[z]["acc20"][:, 0, :], "scalar")
+        store(z, 2, 1)

@@ -335,8 +335,8 @@ def tile_symbolicpenaltytracker_kernel(tc, A_rel, k_seq, out):
             if n + AHEAD < B:
                 load_a(n + AHEAD)
                 load_k(n + AHEAD)
-            if n + 2 < B:
-                regroup_k(n + 2)
+            if n > 0:
+                regroup_k(n + 1)
             if n > 0:
                 invert(n + 1, EVERY)
                 spread(n + 1, ALL)
@@ -356,9 +356,6 @@ def tile_symbolicpenaltytracker_kernel(tc, A_rel, k_seq, out):
             copy_w(n, 1)
             if n % 2:
                 copy_w(n, "shared")
-            if n == 0:
-                quantise_k(0)
-                move_k(0)
             largest_3(n)
             if n == 0:
                 invert(1, EVERY)
@@ -369,10 +366,14 @@ def tile_symbolicpenaltytracker_kernel(tc, A_rel, k_seq, out):
             if n > 0:
                 quantise_w(n - 1)
                 products(n - 1)
+            if n == 0:
+                quantise_k(0)
+                move_k(0)
             quantise_k(n + 1)
             move_k(n + 1)
         y = B - 2
         z = B - 1
+        regroup_k(z)
         invert(z, EVERY)
         spread(z, ALL)
         for i in (3, 2, 0, 1):

@@ -29,6 +29,7 @@ SUMS_ON_VECTOR = (0,)
 AHEAD = 4
 N_KA = 3
 N_KB = 2
+N_QS = 4
 W_FIRST = ({3: 0, 2: 512, 0: 896, 1: 1024}, {1: 1280, 2: 1536, 0: 1920, 3: 2048})
 W_SHARED = 1024
 W_PAIR = 2560
@@ -80,9 +81,9 @@ def tile_symbolicpenaltytracker_kernel(tc, A_rel, k_seq, out):
         ident_f = const.tile([P, P], F32, name="ident_f")
         make_identity(nc, ident_f[:])
 
-        kc = [const.tile([P, D], U32, name="kc%d" % b, align_bytes=64) for b in range(B)]
+        kc = [const.tile([P, D], U32, name="kc%d" % b, align_bytes=64) for b in range(2)]
         kz = const.tile([P, N_KA + N_KB, 2, D], U32, name="kz", align_bytes=64)
-        planes = const.tile([P, 2 * (N_KA + N_KB) + B, D], U8, name="planes", align_bytes=64)
+        planes = const.tile([P, 2 * (N_KA + N_KB) + 2 + 2 * N_QS, D], U8, name="planes", align_bytes=64)
         nc.vector.memset(kz[:, 0:N_KA, :, :].rearrange("p j h d -> p (j h d)").bitcast(I32), 0)
         nc.gpsimd.memset(planes[:].rearrange("p b d -> p (b d)").bitcast(I32), 0)
         nc.gpsimd.memset(kz[:, N_KA:, :, :].rearrange("p j h d -> p (j h d)").bitcast(I32), 0)
@@ -90,7 +91,8 @@ def tile_symbolicpenaltytracker_kernel(tc, A_rel, k_seq, out):
         kb = [kz[:, N_KA + j, :, :] for j in range(N_KB)]
         ka_s = [planes[:, 2 * j : 2 * j + 2, :] for j in range(N_KA)]
         kb_s = [planes[:, 2 * (N_KA + j) : 2 * (N_KA + j) + 2, :] for j in range(N_KB)]
-        ks = planes[:, 2 * (N_KA + N_KB) :, :]
+        ks = planes[:, 2 * (N_KA + N_KB) : 2 * (N_KA + N_KB) + 2, :]
+        qs = [planes[:, 2 * (N_KA + N_KB + 1 + j) : 2 * (N_KA + N_KB + 2 + j), :] for j in range(N_QS)]
 
         state = [{} for b in range(B)]
         ALL = list(range(NB))
@@ -100,11 +102,26 @@ def tile_symbolicpenaltytracker_kernel(tc, A_rel, k_seq, out):
                 state[b][name] = make()
             return state[b][name]
 
+        def qin(b):
+            return tile_of(
+                b, "qin", lambda: work.tile([P, 2, 2 * P * PACK], BF16, name="qin", align_bytes=64)
+            )
+
+        def k_codes(b):
+            return kc[b][:] if b < 2 else state[b - 2]["qc"][:, 1, :]
+
+        def k_scales(b):
+            return ks[:, b, :] if b < 2 else qs[(b - 2) % N_QS][:, 1, :]
+
         def regroup_k(b):
-            kg = work.tile([P, D * PACK], BF16, name="kg", align_bytes=64)
-            state[b]["kg"] = kg
+            if b < 2:
+                kg = work.tile([P, D * PACK], BF16, name="kg", bufs=2, align_bytes=64)
+                state[b]["kg"] = kg
+                dst = kg[:]
+            else:
+                dst = qin(b - 2)[:, 1, :]
             nc.gpsimd.tensor_scalar(
-                out=kg[:].rearrange("p (d u) -> p d u", u=PACK),
+                out=dst.rearrange("p (d u) -> p d u", u=PACK),
                 in0=k_sb[b][:].rearrange("p u d -> p d u"),
                 scalar1=1.0, scalar2=0.0, op0=ALU.mult, op1=ALU.add,
             )
@@ -115,10 +132,10 @@ def tile_symbolicpenaltytracker_kernel(tc, A_rel, k_seq, out):
         def move_k(b):
             def move(dst, dst_s, half, p0, n):
                 nc.sync.dma_start(
-                    out=dst[p0 : p0 + n, half, :].bitcast(I32), in_=kc[b][0:n, :].bitcast(I32)
+                    out=dst[p0 : p0 + n, half, :].bitcast(I32), in_=k_codes(b)[0:n, :].bitcast(I32)
                 )
                 nc.sync.dma_start(
-                    out=dst_s[p0 : p0 + n, half, :].bitcast(I32), in_=ks[0:n, b, :].bitcast(I32)
+                    out=dst_s[p0 : p0 + n, half, :].bitcast(I32), in_=k_scales(b)[0:n, :].bitcast(I32)
                 )
 
             j = b % N_KA
@@ -194,10 +211,7 @@ def tile_symbolicpenaltytracker_kernel(tc, A_rel, k_seq, out):
                 state[b]["groupedb"] = work.tile([P, P * PACK], BF16, name="groupedb", bufs=2, align_bytes=64)
                 dst = state[b]["groupedb"][:]
             else:
-                grouped = tile_of(
-                    b, "grouped", lambda: work.tile([P, 2, P * PACK], BF16, name="grouped", align_bytes=64)
-                )
-                dst = grouped[:, tile, :]
+                dst = qin(b)[:, 0, tile * P * PACK : (tile + 1) * P * PACK]
             nc.scalar.copy(
                 out=dst.rearrange("p (t u) -> p t u", u=PACK),
                 in_=state[b]["wt", tile][:].rearrange("p u t -> p t u"),
@@ -244,12 +258,13 @@ def tile_symbolicpenaltytracker_kernel(tc, A_rel, k_seq, out):
             )
 
         def quantise_main(b, tiles):
-            codes = tile_of(b, "wc", lambda: work.tile([P, 2 * P], U32, name="wc", align_bytes=64))
-            scales = tile_of(b, "ws", lambda: work.tile([P, 2 * P], U8, name="ws", align_bytes=64))
-            c = slice(tiles[0] * P, (tiles[-1] + 1) * P)
+            codes = tile_of(b, "qc", lambda: work.tile([P, 2, D], U32, name="qc", bufs=4, align_bytes=64))
+            scales = qs[b % N_QS]
+            c = slice(tiles[0] * P, (2 * D if b + 2 < B else (tiles[-1] + 1) * P))
             nc.vector.quantize_mx(
-                out=codes[:, c].bitcast(FP8X4), scales=scales[:, c],
-                in_=state[b]["grouped"][:].rearrange("p j x -> p (j x)")[:, c.start * PACK : c.stop * PACK],
+                out=codes[:].rearrange("p h d -> p (h d)")[:, c].bitcast(FP8X4),
+                scales=scales.rearrange("p h d -> p (h d)")[:, c],
+                in_=qin(b)[:].rearrange("p h x -> p (h x)")[:, c.start * PACK : c.stop * PACK],
             )
 
         def quantise_shared(b):
@@ -261,14 +276,15 @@ def tile_symbolicpenaltytracker_kernel(tc, A_rel, k_seq, out):
         def product_3(b):
             s = state[b]
             s["acc3"] = ps_out.tile([P, 2, D], F32, name="acc")
-            mx(s["acc3"][:, 0, :], s["wc"][:, 0:P], s["ws"][:, 0:P], kc[b][:], ks[:, b, :])
+            w, w_s = s["qc"][:, 0, 0:P], qs[b % N_QS][:, 0, 0:P]
+            mx(s["acc3"][:, 0, :], w, w_s, k_codes(b), k_scales(b))
 
         def product_20(b):
             s = state[b]
             s["acc20"] = ps_out.tile([P, 2, D], F32, name="acc")
             j = b % N_KA
             mx(
-                s["acc20"][:].rearrange("p h d -> p (h d)"), s["wc"][:, P : 2 * P], s["ws"][:, P : 2 * P],
+                s["acc20"][:].rearrange("p h d -> p (h d)"), s["qc"][:, 0, P : 2 * P], qs[b % N_QS][:, 0, P : 2 * P],
                 ka[j].rearrange("p h d -> p (h d)"), ka_s[j].rearrange("p h d -> p (h d)"),
             )
 
@@ -309,21 +325,24 @@ def tile_symbolicpenaltytracker_kernel(tc, A_rel, k_seq, out):
         LO = slice(0, 2)
         HI = slice(2, 4)
 
-        for i in ALL:
-            row_sum(0, i, ("scalar", "vector")[i % 2])
-            if i == 1:
-                root(0, LO)
-        root(0, HI)
+        row_sum(0, 0, "scalar")
+        row_sum(0, 1, "vector")
+        root(0, LO)
+        row_sum(0, 2, "scalar")
         mask(0, [1])
-        mask(0, [3])
         invert(0, LO)
         spread(0, [0, 1])
+        row_sum(0, 3, "vector")
+        root(0, HI)
+        mask(0, [3])
         mask(0, [0])
         multiply(0, 0)
         multiply(0, 1)
         invert(0, HI)
         spread(0, [2, 3])
         mask(0, [2])
+        largest(0, 0)
+        largest(0, 1)
         multiply(0, 2)
         multiply(0, 3)
         for i in ALL:
@@ -349,10 +368,10 @@ def tile_symbolicpenaltytracker_kernel(tc, A_rel, k_seq, out):
             if n + 2 < B:
                 for i in ALL:
                     row_sum(n + 2, i, "vector" if i in SUMS_ON_VECTOR else "scalar")
-                root(n + 2, EVERY)
             if n > 1:
                 outputs(n - 2)
             copy_w(n, 0)
+            root(n + 2, EVERY)
             copy_w(n, 1)
             if n % 2:
                 copy_w(n, "shared")
@@ -361,15 +380,16 @@ def tile_symbolicpenaltytracker_kernel(tc, A_rel, k_seq, out):
                 invert(1, EVERY)
                 spread(1, ALL)
             mask(n + 1, ALL)
-            largest_210(n)
+            for i in (2, 1, 0) if n > 0 else (2,):
+                largest(n, i)
             factors(n)
-            if n > 0:
-                quantise_w(n - 1)
-                products(n - 1)
             if n == 0:
                 quantise_k(0)
                 move_k(0)
-            quantise_k(n + 1)
+                quantise_k(1)
+            else:
+                quantise_w(n - 1)
+                products(n - 1)
             move_k(n + 1)
         y = B - 2
         z = B - 1
@@ -383,11 +403,10 @@ def tile_symbolicpenaltytracker_kernel(tc, A_rel, k_seq, out):
         outputs(y - 2)
         copy_w(y, 0)
         copy_w(y, 1)
-        quantise_k(z)
-        move_k(z)
         mask(z, ALL)
         quantise_w(y - 1)
         products(y - 1)
+        move_k(z)
         outputs(y - 1)
         multiply(z, 1)
         turn(z, "shared")
@@ -420,7 +439,7 @@ def tile_symbolicpenaltytracker_kernel(tc, A_rel, k_seq, out):
         store(z, 1, 1)
         scale_out(z, 3, state[z]["acc3"][:, 0, :], "scalar")
         store(z, 3, 1)
-        scale_out(z, 0, state[z]["acc20"][:, 1, :], "vector")
-        store(z, 0, 1)
         scale_out(z, 2, state[z]["acc20"][:, 0, :], "scalar")
         store(z, 2, 1)
+        scale_out(z, 0, state[z]["acc20"][:, 1, :], "scalar")
+        store(z, 0, 1)

import math
from contextlib import ExitStack

import concourse.mybir as mybir
from concourse.masks import make_identity

F32 = mybir.dt.float32
BF16 = mybir.dt.bfloat16
I32 = mybir.dt.int32
U32 = mybir.dt.uint32
U8 = mybir.dt.uint8
FP8X4 = mybir.dt.float8_e4m3fn_x4
ALU = mybir.AluOpType
ACT = mybir.ActivationFunctionType
AX = mybir.AxisListType

B, T, D = 8, 512, 256
P = 128
NB = T // P
PACK = 4
Q = P // PACK
GAMMA = 0.5
EPS = 1e-06
REL_THRESH = 1e-09
FLOPS = 2 * B * T * T * D

DIAG_STEP = T + P
SUMS_ON_VECTOR = (0,)
AHEAD = 4
N_KA = 3
N_KB = 2
N_QS = 4
W_FIRST = ({3: 0, 2: 512, 0: 896, 1: 1024}, {1: 1280, 2: 1536, 0: 1920, 3: 2048})
W_SHARED = 1024
W_PAIR = 2560


def tile_symbolicpenaltytracker_kernel(tc, A_rel, k_seq, out):
    nc = tc.nc
    with ExitStack() as ctx:
        const = ctx.enter_context(tc.tile_pool(name="const", bufs=1))
        resid = ctx.enter_context(tc.tile_pool(name="resid", bufs=1))
        small = ctx.enter_context(tc.tile_pool(name="small", bufs=4))
        work = ctx.enter_context(tc.tile_pool(name="work", bufs=3))
        ps_dis = ctx.enter_context(tc.psum_pool(name="ps_dis", bufs=2))
        ps_wt = ctx.enter_context(tc.psum_pool(name="ps_wt", bufs=3))
        ps_out = ctx.enter_context(tc.psum_pool(name="ps_out", bufs=3))

        a_sb = [resid.tile([P, NB * DIAG_STEP], BF16, name="a%d" % b) for b in range(B)]
        k_sb = [resid.tile([P, PACK, D], BF16, name="k%d" % b) for b in range(B)]

        def rows(b):
            return a_sb[b][:, 0 : NB * T].rearrange("p (i s) -> p i s", s=T)

        def load_a(b):
            if b == 0:
                for i in range(NB):
                    nc.sync.dma_start(out=rows(b)[:, i, :], in_=A_rel[b, i * P : (i + 1) * P, :])
            else:
                nc.sync.dma_start(out=rows(b), in_=A_rel[b].rearrange("(i p) s -> p i s", p=P))

        def load_k(b):
            nc.sync.dma_start(out=k_sb[b][:], in_=k_seq[b].rearrange("(p u) d -> p u d", u=PACK))

        load_a(0)
        for b in range(1, AHEAD):
            load_a(b)
            load_k(b - 1)
        load_k(AHEAD - 1)

        warm = const.tile([P, 1], F32, name="warm")
        nc.vector.memset(warm[:], 1.0)
        nc.scalar.activation(out=warm[:], in_=warm[:], func=ACT.Sqrt)

        tril = const.tile([P, P], BF16, name="tril")
        nc.gpsimd.memset(tril[:], 1.0)
        nc.gpsimd.affine_select(
            out=tril[:], in_=tril[:], compare_op=ALU.is_ge, fill=0.0, base=0,
            pattern=[[-1, P]], channel_multiplier=1,
        )
        ident_f = const.tile([P, P], F32, name="ident_f")
        make_identity(nc, ident_f[:])

        kc = [const.tile([P, D], U32, name="kc%d" % b, align_bytes=64) for b in range(2)]
        kz = const.tile([P, N_KA + N_KB, 2, D], U32, name="kz", align_bytes=64)
        planes = const.tile([P, 2 * (N_KA + N_KB) + 2 + 2 * N_QS, D], U8, name="planes", align_bytes=64)
        nc.vector.memset(kz[:, 0:N_KA, :, :].rearrange("p j h d -> p (j h d)").bitcast(I32), 0)
        nc.gpsimd.memset(planes[:].rearrange("p b d -> p (b d)").bitcast(I32), 0)
        nc.gpsimd.memset(kz[:, N_KA:, :, :].rearrange("p j h d -> p (j h d)").bitcast(I32), 0)
        ka = [kz[:, j, :, :] for j in range(N_KA)]
        kb = [kz[:, N_KA + j, :, :] for j in range(N_KB)]
        ka_s = [planes[:, 2 * j : 2 * j + 2, :] for j in range(N_KA)]
        kb_s = [planes[:, 2 * (N_KA + j) : 2 * (N_KA + j) + 2, :] for j in range(N_KB)]
        ks = planes[:, 2 * (N_KA + N_KB) : 2 * (N_KA + N_KB) + 2, :]
        qs = [planes[:, 2 * (N_KA + N_KB + 1 + j) : 2 * (N_KA + N_KB + 2 + j), :] for j in range(N_QS)]

        state = [{} for b in range(B)]
        ALL = list(range(NB))

        def tile_of(b, name, make):
            if name not in state[b]:
                state[b][name] = make()
            return state[b][name]

        def qin(b):
            return tile_of(
                b, "qin", lambda: work.tile([P, 2, 2 * P * PACK], BF16, name="qin", align_bytes=64)
            )

        def k_codes(b):
            return kc[b][:] if b < 2 else state[b - 2]["qc"][:, 1, :]

        def k_scales(b):
            return ks[:, b, :] if b < 2 else qs[(b - 2) % N_QS][:, 1, :]

        def regroup_k(b):
            if b < 2:
                kg = work.tile([P, D * PACK], BF16, name="kg", bufs=2, align_bytes=64)
                state[b]["kg"] = kg
                dst = kg[:]
            else:
                dst = qin(b - 2)[:, 1, :]
            nc.gpsimd.tensor_scalar(
                out=dst.rearrange("p (d u) -> p d u", u=PACK),
                in0=k_sb[b][:].rearrange("p u d -> p d u"),
                scalar1=1.0, scalar2=0.0, op0=ALU.mult, op1=ALU.add,
            )

        def quantise_k(b):
            nc.vector.quantize_mx(out=kc[b][:].bitcast(FP8X4), scales=ks[:, b, :], in_=state[b]["kg"][:])

        def move_k(b):
            def move(dst, dst_s, half, p0, n):
                nc.sync.dma_start(
                    out=dst[p0 : p0 + n, half, :].bitcast(I32), in_=k_codes(b)[0:n, :].bitcast(I32)
                )
                nc.sync.dma_start(
                    out=dst_s[p0 : p0 + n, half, :].bitcast(I32), in_=k_scales(b)[0:n, :].bitcast(I32)
                )

            j = b % N_KA
            move(ka[j], ka_s[j], 0, 0, 3 * Q)
            move(ka[j], ka_s[j], 1, 3 * Q, Q)
            m = (b // 2) % N_KB
            move(kb[m], kb_s[m], b % 2, (b % 2) * 2 * Q, 2 * Q)

        def row_sum(b, i, engine):
            deg = tile_of(b, "deg", lambda: small.tile([P, NB], F32, name="deg"))
            if engine == "vector":
                unused = work.tile([P, T], BF16, name="unused_v")
                nc.vector.tensor_scalar(
                    out=unused[:], in0=rows(b)[:, i, :], scalar1=1.0, scalar2=None,
                    op0=ALU.mult, op1=ALU.add, accum_out=deg[:, i : i + 1],
                )
            else:
                unused = work.tile([P, T], BF16, name="unused_s")
                nc.scalar.activation(
                    out=unused[:], in_=rows(b)[:, i, :], func=ACT.Copy, accum_out=deg[:, i : i + 1]
                )

        def root(b, c):
            sd = tile_of(b, "sd", lambda: small.tile([P, NB], F32, name="sd"))
            nc.scalar.activation(out=sd[:, c], in_=state[b]["deg"][:, c], func=ACT.Sqrt, bias=EPS)

        def invert(b, c):
            dis = tile_of(b, "dis", lambda: small.tile([P, NB], F32, name="dis"))
            nc.vector.reciprocal(out=dis[:, c], in_=state[b]["sd"][:, c])

        def spread(b, blocks):
            dis_all = tile_of(b, "dis_all", lambda: ps_dis.tile([P, T], F32, name="dis_all"))
            for i in blocks:
                nc.tensor.transpose(
                    out=dis_all[:, i * P : (i + 1) * P],
                    in_=state[b]["dis"][:, i : i + 1].to_broadcast([P, P]),
                    identity=ident_f[:],
                )

        def mask(b, blocks):
            if len(blocks) == 1:
                i = blocks[0]
                diag = rows(b)[:, i, i * P : (i + 1) * P]
                nc.vector.tensor_tensor(out=diag, in0=diag, in1=tril[:], op=ALU.mult)
            else:
                diag = a_sb[b][:].rearrange("p (i x) -> p i x", x=DIAG_STEP)[:, :, 0:P]
                nc.vector.tensor_tensor(
                    out=diag, in0=diag, in1=tril[:].unsqueeze(1).to_broadcast([P, NB, P]), op=ALU.mult
                )

        def w32(b, i):
            pair = tile_of(b - b % 2, "w32", lambda: work.tile([P, W_PAIR], F32, name="w32", bufs=2))
            first = W_FIRST[b % 2][i]
            return pair[:, first : first + (i + 1) * P]

        def multiply(b, i):
            n = (i + 1) * P
            nc.vector.scalar_tensor_tensor(
                out=w32(b, i), in0=rows(b)[:, i, 0:n], scalar=state[b]["dis"][:, i : i + 1],
                in1=state[b]["dis_all"][:, 0:n], op0=ALU.mult, op1=ALU.mult,
            )

        def turn(b, tile):
            wt = ps_wt.tile([P, PACK, P], F32, name="wt")
            state[b]["wt", tile] = wt
            first = W_SHARED if tile == "shared" else W_FIRST[b % 2][(3, 2)[tile]]
            w = state[b - b % 2]["w32"][:, first : first + T]
            for u in range(PACK):
                nc.tensor.transpose(out=wt[:, u, :], in_=w[:, u::PACK], identity=ident_f[:])

        def copy_w(b, tile):
            if tile == "shared":
                state[b]["groupedb"] = work.tile([P, P * PACK], BF16, name="groupedb", bufs=2, align_bytes=64)
                dst = state[b]["groupedb"][:]
            else:
                dst = qin(b)[:, 0, tile * P * PACK : (tile + 1) * P * PACK]
            nc.scalar.copy(
                out=dst.rearrange("p (t u) -> p t u", u=PACK),
                in_=state[b]["wt", tile][:].rearrange("p u t -> p t u"),
            )

        def largest(b, i):
            top = tile_of(b, "top", lambda: small.tile([P, NB], F32, name="top"))
            nc.vector.tensor_reduce(
                out=top[:, i : i + 1], in_=w32(b, i), axis=AX.X, op=ALU.max, apply_absolute_value=True
            )

        def largest_3(b):
            largest(b, 3)

        def largest_210(b):
            for i in (2, 1, 0):
                largest(b, i)

        def factors(b):
            fac = small.tile([P, NB], F32, name="fac")
            engine = nc.gpsimd
            engine.tensor_scalar(
                out=fac[:], in0=state[b]["top"][:], scalar1=REL_THRESH, scalar2=math.sqrt(GAMMA),
                op0=ALU.is_gt, op1=ALU.mult,
            )
            state[b]["fac"] = [fac[:, i : i + 1] for i in ALL]

        def scale_out(b, i, acc, engine):
            res = tile_of(b, "res", lambda: work.tile([P, NB, D], F32, name="res", bufs=4))
            fac = state[b]["fac"][i]
            if engine == "scalar":
                nc.scalar.activation(out=res[:, i, :], in_=acc, func=ACT.Copy, scale=fac)
            else:
                nc.vector.tensor_scalar_mul(out=res[:, i, :], in0=acc, scalar1=fac)

        def store(b, i0, n):
            dst = out[b].rearrange("(i p) d -> p i d", p=P)
            nc.sync.dma_start(out=dst[:, i0 : i0 + n, :], in_=state[b]["res"][:, i0 : i0 + n, :])

        def mx(dst, lhs, lhs_s, rhs, rhs_s):
            nc.tensor.matmul_mx(
                out=dst, lhsT=lhs.bitcast(FP8X4), lhsT_scale=lhs_s, rhs=rhs.bitcast(FP8X4), rhs_scale=rhs_s,
                start=True, stop=True,
            )

        def quantise_main(b, tiles):
            codes = tile_of(b, "qc", lambda: work.tile([P, 2, D], U32, name="qc", bufs=4, align_bytes=64))
            scales = qs[b % N_QS]
            c = slice(tiles[0] * P, (2 * D if b + 2 < B else (tiles[-1] + 1) * P))
            nc.vector.quantize_mx(
                out=codes[:].rearrange("p h d -> p (h d)")[:, c].bitcast(FP8X4),
                scales=scales.rearrange("p h d -> p (h d)")[:, c],
                in_=qin(b)[:].rearrange("p h x -> p (h x)")[:, c.start * PACK : c.stop * PACK],
            )

        def quantise_shared(b):
            s = state[b]
            s["wcb"] = work.tile([P, P], U32, name="wcb", bufs=2, align_bytes=64)
            s["wsb"] = work.tile([P, P], U8, name="wsb", bufs=2, align_bytes=64)
            nc.vector.quantize_mx(out=s["wcb"][:].bitcast(FP8X4), scales=s["wsb"][:], in_=s["groupedb"][:])

        def product_3(b):
            s = state[b]
            s["acc3"] = ps_out.tile([P, 2, D], F32, name="acc")
            w, w_s = s["qc"][:, 0, 0:P], qs[b % N_QS][:, 0, 0:P]
            mx(s["acc3"][:, 0, :], w, w_s, k_codes(b), k_scales(b))

        def product_20(b):
            s = state[b]
            s["acc20"] = ps_out.tile([P, 2, D], F32, name="acc")
            j = b % N_KA
            mx(
                s["acc20"][:].rearrange("p h d -> p (h d)"), s["qc"][:, 0, P : 2 * P], qs[b % N_QS][:, 0, P : 2 * P],
                ka[j].rearrange("p h d -> p (h d)"), ka_s[j].rearrange("p h d -> p (h d)"),
            )

        def product_shared(b):
            s = state[b]
            s["acc1"] = ps_out.tile([P, 2, D], F32, name="acc")
            m = (b // 2) % N_KB
            mx(
                s["acc1"][:].rearrange("p h d -> p (h d)"), s["wcb"][:], s["wsb"][:],
                kb[m].rearrange("p h d -> p (h d)"), kb_s[m].rearrange("p h d -> p (h d)"),
            )

        def quantise_w(b):
            quantise_main(b, (0, 1))
            if b % 2:
                quantise_shared(b)

        def products(b):
            product_3(b)
            product_20(b)
            if b % 2:
                product_shared(b)

        def outputs(b):
            s = state[b]
            scale_out(b, 3, s["acc3"][:, 0, :], "scalar")
            scale_out(b, 2, s["acc20"][:, 0, :], "scalar")
            store(b, 2, 2)
            scale_out(b, 0, s["acc20"][:, 1, :], "scalar")
            if b % 2:
                scale_out(b - 1, 1, s["acc1"][:, 0, :], "scalar")
                store(b - 1, 0, 2)
                scale_out(b, 1, s["acc1"][:, 1, :], "scalar")
                store(b, 0, 2)

        ctx.enter_context(tc.manual_schedule())
        EVERY = slice(0, NB)
        LO = slice(0, 2)
        HI = slice(2, 4)

        row_sum(0, 0, "scalar")
        row_sum(0, 1, "vector")
        root(0, LO)
        row_sum(0, 2, "scalar")
        mask(0, [1])
        invert(0, LO)
        spread(0, [0, 1])
        row_sum(0, 3, "vector")
        root(0, HI)
        mask(0, [3])
        mask(0, [0])
        multiply(0, 0)
        multiply(0, 1)
        invert(0, HI)
        spread(0, [2, 3])
        mask(0, [2])
        largest(0, 0)
        largest(0, 1)
        multiply(0, 2)
        multiply(0, 3)
        for i in ALL:
            row_sum(1, i, "scalar")
        root(1, EVERY)
        regroup_k(0)
        regroup_k(1)
        for n in range(B - 2):
            if n + AHEAD < B:
                load_a(n + AHEAD)
                load_k(n + AHEAD)
            if n > 0:
                regroup_k(n + 1)
            if n > 0:
                invert(n + 1, EVERY)
                spread(n + 1, ALL)
                for i in (3, 2, 0, 1):
                    multiply(n, i)
            turn(n, 0)
            turn(n, 1)
            if n % 2:
                turn(n, "shared")
            if n + 2 < B:
                for i in ALL:
                    row_sum(n + 2, i, "vector" if i in SUMS_ON_VECTOR else "scalar")
            if n > 1:
                outputs(n - 2)
            copy_w(n, 0)
            root(n + 2, EVERY)
            copy_w(n, 1)
            if n % 2:
                copy_w(n, "shared")
            largest_3(n)
            if n == 0:
                invert(1, EVERY)
                spread(1, ALL)
            mask(n + 1, ALL)
            for i in (2, 1, 0) if n > 0 else (2,):
                largest(n, i)
            factors(n)
            if n == 0:
                quantise_k(0)
                move_k(0)
                quantise_k(1)
            else:
                quantise_w(n - 1)
                products(n - 1)
            move_k(n + 1)
        y = B - 2
        z = B - 1
        regroup_k(z)
        invert(z, EVERY)
        spread(z, ALL)
        for i in (3, 2, 0, 1):
            multiply(y, i)
        turn(y, 0)
        turn(y, 1)
        outputs(y - 2)
        copy_w(y, 0)
        copy_w(y, 1)
        mask(z, ALL)
        quantise_w(y - 1)
        products(y - 1)
        move_k(z)
        outputs(y - 1)
        multiply(z, 1)
        turn(z, "shared")
        multiply(z, 3)
        turn(z, 0)
        largest_3(y)
        quantise_w(y)
        products(y)
        largest_210(y)
        factors(y)
        copy_w(z, "shared")
        copy_w(z, 0)
        multiply(z, 2)
        multiply(z, 0)
        turn(z, 1)
        outputs(y)
        copy_w(z, 1)
        largest_210(z)
        quantise_shared(z)
        product_shared(z)
        largest_3(z)
        factors(z)
        quantise_main(z, (0,))
        product_3(z)
        scale_out(y, 1, state[z]["acc1"][:, 0, :], "scalar")
        store(y, 0, 2)
        quantise_main(z, (1,))
        product_20(z)
        scale_out(z, 1, state[z]["acc1"][:, 1, :], "vector")
        store(z, 1, 1)
        scale_out(z, 3, state[z]["acc3"][:, 0, :], "scalar")
        store(z, 3, 1)
        scale_out(z, 2, state[z]["acc20"][:, 0, :], "scalar")
        store(z, 2, 1)
        scale_out(z, 0, state[z]["acc20"][:, 1, :], "scalar")
        store(z, 0, 1)
